import numpy as np
import ml_dtypes


def mxq(x, axis, fmt="e4m3"):
    dtype, down = {"e4m3": (ml_dtypes.float8_e4m3fn, 7), "e5m2": (ml_dtypes.float8_e5m2, 14)}[fmt]
    v = np.moveaxis(np.asarray(x, np.float32).astype(ml_dtypes.bfloat16).astype(np.float64), axis, -1)
    blocks = v.reshape(v.shape[:-1] + (-1, 32))
    amax = np.abs(blocks).max(-1, keepdims=True)
    byte = np.maximum(np.where(amax > 0, np.frexp(amax)[1] - 1 + 127, 0) - down, 1)
    scale = np.exp2(byte - 127.0)
    codes = (blocks / scale).astype(np.float32).astype(dtype).astype(np.float64)
    return np.moveaxis((codes * scale).reshape(v.shape), -1, axis)


WIDE = False


def mx_kscale(k):
    if not WIDE:
        return np.ones(k)
    levels = np.array([10, -10, 5, -5, 0])
    a = np.random.permutation(np.resize(levels, k // 512 * 4)).reshape(k // 512, 4)
    idx = np.arange(k)
    return np.exp2(a[idx // 512, idx % 128 // 32])


BF16 = ml_dtypes.bfloat16


def bf(x):
    return np.asarray(x, np.float32).astype(BF16)


def f64(x):
    return np.asarray(x).astype(np.float64)


B, IN, HID, BLK, OUT = 512, 1024, 4096, 512, 10
NB = HID // BLK


def setup_inputs():
    s = mx_kscale(IN)
    t = np.tile(mx_kscale(BLK), NB)
    return {
        "x": bf(np.random.standard_normal((B, IN)) * s),
        "W1": bf(np.random.standard_normal((HID, IN)) / np.sqrt(IN) / s * t[:, None]),
        "b1": bf(np.random.standard_normal(HID) * 0.3 * t),
        "Wb": bf(np.random.standard_normal((NB, BLK, BLK)) * 1.4 / np.sqrt(BLK) / t.reshape(NB, 1, BLK)),
        "bb": bf(np.random.standard_normal(HID) * 0.3),
    }


def reference(x, W1, b1, Wb, bb):
    h = np.maximum((mxq(f64(x), 1, "e4m3") @ mxq(f64(W1), 1, "e4m3").T) + f64(b1), 0.0)
    hb = h.reshape(B, NB, BLK)
    yb = (mxq(hb, 2, "e4m3").transpose(1, 0, 2) @ mxq(f64(Wb), 2, "e4m3").transpose(0, 2, 1)).transpose(1, 0, 2)
    return np.maximum(yb.reshape(B, HID) + f64(bb), 0.0)

@@ -1,0 +1,243 @@
+from contextlib import ExitStack
+
+import concourse.mybir as mybir
+from concourse.masks import make_identity
+
+F32 = mybir.dt.float32
+BF16 = mybir.dt.bfloat16
+U32 = mybir.dt.uint32
+U8 = mybir.dt.uint8
+FP8X4 = mybir.dt.float8_e4m3fn_x4
+RELU = mybir.ActivationFunctionType.Relu
+ADD = mybir.AluOpType.add
+
+P = 128
+B = 512
+IN = 1024
+HID = 4096
+BLK = 512
+NB = 8
+FLOPS = 2 * B * IN * HID + 2 * B * BLK * HID
+
+
+def tile_blockdiagmnistconvertible_pa_kernel(tc, x, W1, b1, Wb, bb, out):
+    nc = tc.nc
+    with ExitStack() as ctx:
+        const = ctx.enter_context(tc.tile_pool(name="const", bufs=1))
+        w1_pool = ctx.enter_context(tc.tile_pool(name="w1_pool", bufs=NB))
+        wb_pool = ctx.enter_context(tc.tile_pool(name="wb_pool", bufs=NB))
+        grp = ctx.enter_context(tc.tile_pool(name="grp", bufs=2))
+        codes = ctx.enter_context(tc.tile_pool(name="codes", bufs=3))
+        hid = ctx.enter_context(tc.tile_pool(name="hid", bufs=2))
+        res = ctx.enter_context(tc.tile_pool(name="res", bufs=3))
+        psum_t = ctx.enter_context(tc.psum_pool(name="psum_t", bufs=3))
+        psum_h = ctx.enter_context(tc.psum_pool(name="psum_h", bufs=2))
+        psum_o = ctx.enter_context(tc.psum_pool(name="psum_o", bufs=3))
+        ctx.enter_context(tc.manual_schedule())
+
+        ident = const.tile([P, P], F32)
+        make_identity(nc, ident[:])
+        b1w = const.tile([P, 2 * P], BF16)
+        nc.vector.memset(b1w[:], 0.0)
+        bbz = const.tile([P, BLK], BF16)
+        nc.vector.memset(bbz[:], 0.0)
+        nc.sync.dma_start(out=b1w[0:16, :], in_=b1.rearrange("(r w) -> r w", w=2 * P))
+        nc.sync.dma_start(out=bbz[0:NB, :], in_=bb.rearrange("(n o) -> n o", o=BLK))
+
+        x_sb = const.tile([P, 4 * IN], BF16)
+        x_rows = x.rearrange("(p t) k -> p t k", t=4)
+        x_dst = x_sb[:].rearrange("p (t k) -> p t k", t=4)
+        for half in range(2):
+            nc.sync.dma_start(out=x_dst[:, 2 * half:2 * half + 2, :], in_=x_rows[:, 2 * half:2 * half + 2, :])
+
+        w1_sbs = []
+        wb_sbs = []
+        for n in range(NB):
+            w1_sb = w1_pool.tile([P, 4 * IN], BF16)
+            w1_rows = W1[n * BLK:(n + 1) * BLK, :].rearrange("(u p e) k -> p u e k", u=2, p=P, e=2)
+            w1_dst = w1_sb[:].rearrange("p (u e k) -> p u e k", u=2, e=2)
+            if n == 0:
+                for u in range(2):
+                    nc.sync.dma_start(out=w1_dst[:, u, :, :], in_=w1_rows[:, u, :, :])
+            else:
+                nc.sync.dma_start(out=w1_dst, in_=w1_rows)
+            wb_sb = wb_pool.tile([P, 4 * BLK], BF16)
+            nc.sync.dma_start(out=wb_sb[:].rearrange("p (j k) -> p j k", j=4), in_=Wb[n].rearrange("(p j) k -> p j k", j=4))
+            w1_sbs.append(w1_sb)
+            wb_sbs.append(wb_sb)
+
+        identb = const.tile([P, P], BF16)
+        nc.vector.tensor_copy(out=identb[:], in_=ident[:])
+
+        def copy_out(eng, dst, src):
+            if eng == "v":
+                nc.vector.tensor_copy(out=dst, in_=src)
+            else:
+                nc.scalar.copy(out=dst, in_=src)
+
+        def transposes(src32, first_word):
+            bank = psum_t.tile([P, 512], F32)
+            for q in range(4):
+                lo = first_word + P * q
+                nc.tensor.transpose(out=bank[:, P * q:P * (q + 1)], in_=src32[:, lo:lo + P], identity=ident[:])
+            return bank
+
+        b1bank = psum_t.tile([P, 512], F32, tag="bank")
+        nc.tensor.transpose(out=b1bank[:, 0:P], in_=b1w[:].bitcast(F32), identity=ident[:])
+        b1p = const.tile([P, 16], F32)
+        nc.vector.tensor_copy(out=b1p[:], in_=b1bank[:, 0:16])
+        b1f = const.tile([P, 32], F32)
+        nc.vector.tensor_copy(out=b1f[:], in_=b1p[:].bitcast(BF16))
+
+        bbb = const.tile([P, HID], BF16)
+
+        def spread_bb(n, eng):
+            acc = psum_o.tile([P, BLK], F32, tag="acc")
+            nc.tensor.matmul(out=acc[:], lhsT=identb[:, n:n + 1].to_broadcast([P, P]), rhs=bbz[:], start=True, stop=True)
+            copy_out(eng, bbb[:, n * BLK:(n + 1) * BLK], acc[:])
+
+        for n in range(4):
+            spread_bb(n, "vs"[n % 2])
+
+        xg = const.tile([P, 4 * IN], BF16, align_bytes=64)
+        xq = const.tile([P, IN], U32, align_bytes=64)
+        xs = const.tile([P, IN], U8, align_bytes=64)
+        x32 = x_sb[:].bitcast(F32)
+        xg32 = xg[:].bitcast(F32).rearrange("p (g b c u) -> p g b c u", g=2, b=4, u=2)
+        for bt in range(4):
+            bank = transposes(x32, 512 * bt)
+            copy_out("sv"[bt % 2], xg32[:, :, bt, :, :], bank[:].rearrange("p (g u c) -> p g c u", g=2, u=2))
+        for g in range(2):
+            nc.vector.quantize_mx(out=xq[:, g * B:(g + 1) * B].bitcast(FP8X4), scales=xs[:, g * B:(g + 1) * B],
+                                  in_=xg[:, g * 4 * B:(g + 1) * 4 * B])
+
+        w1g = {}
+        wbg = {}
+        w1q = {}
+        w1s = {}
+        wbq = {}
+        wbs = {}
+        hpl = {}
+        hg = {}
+        hq = {}
+        hs = {}
+        ot = {}
+        accs = {}
+
+        def prep(n, engs):
+            w1g_t = grp.tile([P, 4 * IN], BF16, align_bytes=64)
+            wbg_t = grp.tile([P, 4 * BLK], BF16, align_bytes=64)
+            w1g[n] = w1g_t
+            wbg[n] = wbg_t
+            w132 = w1_sbs[n][:].bitcast(F32)
+            g32 = w1g_t[:].bitcast(F32)
+            for j in range(4):
+                bank = transposes(w132, 512 * j)
+                copy_out(engs[j], g32[:, 512 * j:512 * (j + 1)].rearrange("p (g c u) -> p g c u", g=2, u=2),
+                         bank[:].rearrange("p (g u c) -> p g c u", g=2, u=2))
+            wb32 = wb_sbs[n][:].bitcast(F32)
+            b32 = wbg_t[:].bitcast(F32).rearrange("p (c h q) -> p c h q", h=2, q=4)
+            for hb in range(2):
+                bank = transposes(wb32, 512 * hb)
+                copy_out(engs[4 + hb], b32[:, :, hb, :], bank[:].rearrange("p (q c) -> p c q", q=4))
+
+        def quant_w1(n):
+            w1q_t = codes.tile([P, IN], U32, align_bytes=64)
+            w1s_t = codes.tile([P, IN], U8, align_bytes=64)
+            w1q[n] = w1q_t
+            w1s[n] = w1s_t
+            nc.vector.quantize_mx(out=w1q_t[:].bitcast(FP8X4), scales=w1s_t[:], in_=w1g[n][:])
+
+        def quant_wb(n):
+            wbq_t = codes.tile([P, BLK], U32, align_bytes=64)
+            wbs_t = codes.tile([P, BLK], U8, align_bytes=64)
+            wbq[n] = wbq_t
+            wbs[n] = wbs_t
+            nc.vector.quantize_mx(out=wbq_t[:].bitcast(FP8X4), scales=wbs_t[:], in_=wbg[n][:])
+
+        def stage1(n, j):
+            if j == 0:
+                hpl_t = hid.tile([P, 4 * B], BF16)
+                hpl[n] = hpl_t
+            hp = psum_h.tile([P, B], F32)
+            for g in range(2):
+                lo = (2 * j + g) * P
+                nc.tensor.matmul_mx(out=hp[:], lhsT=w1q[n][:, lo:lo + P].bitcast(FP8X4), lhsT_scale=w1s[n][:, lo:lo + P],
+                                    rhs=xq[:, g * B:(g + 1) * B].bitcast(FP8X4), rhs_scale=xs[:, g * B:(g + 1) * B],
+                                    start=(g == 0), stop=(g == 1))
+            nc.scalar.activation(out=hpl[n][:, j * B:(j + 1) * B], in_=hp[:], func=RELU,
+                                 bias=b1f[:, 4 * n + j:4 * n + j + 1], scale=1.0)
+
+        def regroup(n):
+            hg_t = hid.tile([P, 4 * B], BF16, align_bytes=64)
+            hg[n] = hg_t
+            nc.vector.tensor_copy(out=hg_t[:].rearrange("p (c i t) -> p c t i", i=4, t=4),
+                                  in_=hpl[n][:].rearrange("p (t c i) -> p c t i", t=4, i=4))
+
+        def quant_h(n):
+            hq_t = hid.tile([P, B], U32, align_bytes=64)
+            hs_t = hid.tile([P, B], U8, align_bytes=64)
+            hq[n] = hq_t
+            hs[n] = hs_t
+            nc.vector.quantize_mx(out=hq_t[:].bitcast(FP8X4), scales=hs_t[:], in_=hg[n][:])
+
+        def stage2(n, bt):
+            acc = psum_o.tile([P, BLK], F32)
+            accs[(n, bt)] = acc
+            nc.tensor.matmul_mx(out=acc[:], lhsT=hq[n][:, bt * P:(bt + 1) * P].bitcast(FP8X4),
+                                lhsT_scale=hs[n][:, bt * P:(bt + 1) * P],
+                                rhs=wbq[n][:].bitcast(FP8X4), rhs_scale=wbs[n][:], start=True, stop=True)
+
+        def add_bias(n, bt):
+            if bt == 0:
+                ot_t = res.tile([P, 4 * BLK], F32)
+                ot[n] = ot_t
+            nc.vector.tensor_tensor(out=ot[n][:, bt * BLK:(bt + 1) * BLK], in0=accs[(n, bt)][:],
+                                    in1=bbb[:, n * BLK:(n + 1) * BLK], op=ADD)
+
+        out_rows = out.rearrange("(c t) o -> c t o", t=4)
+
+        def finish(n):
+            nc.vector.tensor_scalar_max(out=ot[n][:], in0=ot[n][:], scalar1=0.0)
+            nc.sync.dma_start(out=out_rows[:, :, n * BLK:(n + 1) * BLK], in_=ot[n][:].rearrange("p (t o) -> p t o", t=4))
+
+        prep(0, "svsvss")
+        spread_bb(4, "s")
+        spread_bb(5, "s")
+        quant_w1(0)
+        quant_wb(0)
+        spread_bb(6, "v")
+        spread_bb(7, "v")
+
+        for i in range(NB + 1):
+            if i >= 1:
+                for bt in range(3):
+                    add_bias(i - 1, bt)
+            if i < NB:
+                stage1(i, 0)
+                stage1(i, 1)
+            if i >= 1:
+                stage2(i - 1, 3)
+                add_bias(i - 1, 3)
+                finish(i - 1)
+            if i < NB:
+                stage1(i, 2)
+                stage1(i, 3)
+            if i == 0:
+                prep(1, "ssssss")
+            elif i + 2 < NB:
+                prep(i + 2, "ssssss")
+            if i < NB:
+                regroup(i)
+                if i == 0:
+                    quant_h(i)
+                if i + 1 < NB:
+                    quant_w1(i + 1)
+                if i > 0:
+                    quant_h(i)
+                if i + 1 < NB:
+                    quant_wb(i + 1)
+                for bt in range(3):
+                    stage2(i, bt)
+            if i == 0:
+                prep(2, "ssssss")

@@ -26,13 +26,10 @@ def tile_blockdiagmnistconvertible_pa_kernel(tc, x, W1, b1, Wb, bb, out):
         const = ctx.enter_context(tc.tile_pool(name="const", bufs=1))
         w1_pool = ctx.enter_context(tc.tile_pool(name="w1_pool", bufs=NB))
         wb_pool = ctx.enter_context(tc.tile_pool(name="wb_pool", bufs=NB))
-        grp = ctx.enter_context(tc.tile_pool(name="grp", bufs=2))
-        codes = ctx.enter_context(tc.tile_pool(name="codes", bufs=3))
-        hid = ctx.enter_context(tc.tile_pool(name="hid", bufs=2))
-        res = ctx.enter_context(tc.tile_pool(name="res", bufs=3))
-        psum_t = ctx.enter_context(tc.psum_pool(name="psum_t", bufs=3))
-        psum_h = ctx.enter_context(tc.psum_pool(name="psum_h", bufs=2))
-        psum_o = ctx.enter_context(tc.psum_pool(name="psum_o", bufs=3))
+        two = ctx.enter_context(tc.tile_pool(name="two", bufs=2))
+        three = ctx.enter_context(tc.tile_pool(name="three", bufs=3))
+        ring_s = ctx.enter_context(tc.psum_pool(name="ring_s", bufs=4))
+        ring_v = ctx.enter_context(tc.psum_pool(name="ring_v", bufs=4))
         ctx.enter_context(tc.manual_schedule())
 
         ident = const.tile([P, P], F32)
@@ -50,10 +47,12 @@ def tile_blockdiagmnistconvertible_pa_kernel(tc, x, W1, b1, Wb, bb, out):
         for half in range(2):
             nc.sync.dma_start(out=x_dst[:, 2 * half:2 * half + 2, :], in_=x_rows[:, 2 * half:2 * half + 2, :])
 
-        w1_sbs = []
-        wb_sbs = []
-        for n in range(NB):
+        w1_sbs = {}
+        wb_sbs = {}
+
+        def load_w1(n):
             w1_sb = w1_pool.tile([P, 4 * IN], BF16)
+            w1_sbs[n] = w1_sb
             w1_rows = W1[n * BLK:(n + 1) * BLK, :].rearrange("(u p e) k -> p u e k", u=2, p=P, e=2)
             w1_dst = w1_sb[:].rearrange("p (u e k) -> p u e k", u=2, e=2)
             if n == 0:
@@ -61,10 +60,17 @@ def tile_blockdiagmnistconvertible_pa_kernel(tc, x, W1, b1, Wb, bb, out):
                     nc.sync.dma_start(out=w1_dst[:, u, :, :], in_=w1_rows[:, u, :, :])
             else:
                 nc.sync.dma_start(out=w1_dst, in_=w1_rows)
+
+        def load_wb(n):
             wb_sb = wb_pool.tile([P, 4 * BLK], BF16)
+            wb_sbs[n] = wb_sb
             nc.sync.dma_start(out=wb_sb[:].rearrange("p (j k) -> p j k", j=4), in_=Wb[n].rearrange("(p j) k -> p j k", j=4))
-            w1_sbs.append(w1_sb)
-            wb_sbs.append(wb_sb)
+
+        load_w1(0)
+        for n in range(1, NB):
+            load_w1(n)
+            load_wb(n - 1)
+        load_wb(NB - 1)
 
         identb = const.tile([P, P], BF16)
         nc.vector.tensor_copy(out=identb[:], in_=ident[:])
@@ -76,13 +82,13 @@ def tile_blockdiagmnistconvertible_pa_kernel(tc, x, W1, b1, Wb, bb, out):
                 nc.scalar.copy(out=dst, in_=src)
 
         def transposes(src32, first_word):
-            bank = psum_t.tile([P, 512], F32)
+            bank = ring_s.tile([P, 512], F32)
             for q in range(4):
                 lo = first_word + P * q
                 nc.tensor.transpose(out=bank[:, P * q:P * (q + 1)], in_=src32[:, lo:lo + P], identity=ident[:])
             return bank
 
-        b1bank = psum_t.tile([P, 512], F32, tag="bank")
+        b1bank = ring_s.tile([P, 512], F32, tag="bank")
         nc.tensor.transpose(out=b1bank[:, 0:P], in_=b1w[:].bitcast(F32), identity=ident[:])
         b1p = const.tile([P, 16], F32)
         nc.vector.tensor_copy(out=b1p[:], in_=b1bank[:, 0:16])
@@ -91,13 +97,16 @@ def tile_blockdiagmnistconvertible_pa_kernel(tc, x, W1, b1, Wb, bb, out):
 
         bbb = const.tile([P, HID], BF16)
 
-        def spread_bb(n, eng):
-            acc = psum_o.tile([P, BLK], F32, tag="acc")
-            nc.tensor.matmul(out=acc[:], lhsT=identb[:, n:n + 1].to_broadcast([P, P]), rhs=bbz[:], start=True, stop=True)
-            copy_out(eng, bbb[:, n * BLK:(n + 1) * BLK], acc[:])
+        def spread_bb(pair, eng):
+            wide = ring_v.tile([P, 2 * BLK], BF16, tag="acc")
+            for s in range(2):
+                n = 2 * pair + s
+                nc.tensor.matmul(out=wide[:, s * BLK:(s + 1) * BLK], lhsT=identb[:, n:n + 1].to_broadcast([P, P]), rhs=bbz[:],
+                                 start=True, stop=True)
+            copy_out(eng, bbb[:, 2 * pair * BLK:2 * (pair + 1) * BLK], wide[:])
 
-        for n in range(4):
-            spread_bb(n, "vs"[n % 2])
+        spread_bb(0, "v")
+        spread_bb(1, "s")
 
         xg = const.tile([P, 4 * IN], BF16, align_bytes=64)
         xq = const.tile([P, IN], U32, align_bytes=64)
@@ -124,42 +133,44 @@ def tile_blockdiagmnistconvertible_pa_kernel(tc, x, W1, b1, Wb, bb, out):
         ot = {}
         accs = {}
 
-        def prep(n, engs):
-            w1g_t = grp.tile([P, 4 * IN], BF16, align_bytes=64)
-            wbg_t = grp.tile([P, 4 * BLK], BF16, align_bytes=64)
+        def prep_w1(n, engs):
+            w1g_t = two.tile([P, 4 * IN], BF16, align_bytes=64)
             w1g[n] = w1g_t
-            wbg[n] = wbg_t
             w132 = w1_sbs[n][:].bitcast(F32)
             g32 = w1g_t[:].bitcast(F32)
             for j in range(4):
                 bank = transposes(w132, 512 * j)
                 copy_out(engs[j], g32[:, 512 * j:512 * (j + 1)].rearrange("p (g c u) -> p g c u", g=2, u=2),
                          bank[:].rearrange("p (g u c) -> p g c u", g=2, u=2))
+
+        def prep_wb(n):
+            wbg_t = two.tile([P, 4 * BLK], BF16, align_bytes=64)
+            wbg[n] = wbg_t
             wb32 = wb_sbs[n][:].bitcast(F32)
             b32 = wbg_t[:].bitcast(F32).rearrange("p (c h q) -> p c h q", h=2, q=4)
             for hb in range(2):
                 bank = transposes(wb32, 512 * hb)
-                copy_out(engs[4 + hb], b32[:, :, hb, :], bank[:].rearrange("p (q c) -> p c q", q=4))
+                copy_out("s", b32[:, :, hb, :], bank[:].rearrange("p (q c) -> p c q", q=4))
 
         def quant_w1(n):
-            w1q_t = codes.tile([P, IN], U32, align_bytes=64)
-            w1s_t = codes.tile([P, IN], U8, align_bytes=64)
+            w1q_t = three.tile([P, IN], U32, align_bytes=64)
+            w1s_t = three.tile([P, IN], U8, align_bytes=64)
             w1q[n] = w1q_t
             w1s[n] = w1s_t
             nc.vector.quantize_mx(out=w1q_t[:].bitcast(FP8X4), scales=w1s_t[:], in_=w1g[n][:])
 
         def quant_wb(n):
-            wbq_t = codes.tile([P, BLK], U32, align_bytes=64)
-            wbs_t = codes.tile([P, BLK], U8, align_bytes=64)
+            wbq_t = three.tile([P, BLK], U32, align_bytes=64)
+            wbs_t = three.tile([P, BLK], U8, align_bytes=64)
             wbq[n] = wbq_t
             wbs[n] = wbs_t
             nc.vector.quantize_mx(out=wbq_t[:].bitcast(FP8X4), scales=wbs_t[:], in_=wbg[n][:])
 
         def stage1(n, j):
             if j == 0:
-                hpl_t = hid.tile([P, 4 * B], BF16)
+                hpl_t = three.tile([P, 4 * B], BF16)
                 hpl[n] = hpl_t
-            hp = psum_h.tile([P, B], F32)
+            hp = ring_s.tile([P, B], F32, tag="bank")
             for g in range(2):
                 lo = (2 * j + g) * P
                 nc.tensor.matmul_mx(out=hp[:], lhsT=w1q[n][:, lo:lo + P].bitcast(FP8X4), lhsT_scale=w1s[n][:, lo:lo + P],
@@ -169,20 +180,20 @@ def tile_blockdiagmnistconvertible_pa_kernel(tc, x, W1, b1, Wb, bb, out):
                                  bias=b1f[:, 4 * n + j:4 * n + j + 1], scale=1.0)
 
         def regroup(n):
-            hg_t = hid.tile([P, 4 * B], BF16, align_bytes=64)
+            hg_t = two.tile([P, 4 * B], BF16, align_bytes=64)
             hg[n] = hg_t
             nc.vector.tensor_copy(out=hg_t[:].rearrange("p (c i t) -> p c t i", i=4, t=4),
                                   in_=hpl[n][:].rearrange("p (t c i) -> p c t i", t=4, i=4))
 
         def quant_h(n):
-            hq_t = hid.tile([P, B], U32, align_bytes=64)
-            hs_t = hid.tile([P, B], U8, align_bytes=64)
+            hq_t = three.tile([P, B], U32, align_bytes=64)
+            hs_t = three.tile([P, B], U8, align_bytes=64)
             hq[n] = hq_t
             hs[n] = hs_t
             nc.vector.quantize_mx(out=hq_t[:].bitcast(FP8X4), scales=hs_t[:], in_=hg[n][:])
 
         def stage2(n, bt):
-            acc = psum_o.tile([P, BLK], F32)
+            acc = ring_v.tile([P, BLK], F32)
             accs[(n, bt)] = acc
             nc.tensor.matmul_mx(out=acc[:], lhsT=hq[n][:, bt * P:(bt + 1) * P].bitcast(FP8X4),
                                 lhsT_scale=hs[n][:, bt * P:(bt + 1) * P],
@@ -190,7 +201,7 @@ def tile_blockdiagmnistconvertible_pa_kernel(tc, x, W1, b1, Wb, bb, out):
 
         def add_bias(n, bt):
             if bt == 0:
-                ot_t = res.tile([P, 4 * BLK], F32)
+                ot_t = three.tile([P, 4 * BLK], F32)
                 ot[n] = ot_t
             nc.vector.tensor_tensor(out=ot[n][:, bt * BLK:(bt + 1) * BLK], in0=accs[(n, bt)][:],
                                     in1=bbb[:, n * BLK:(n + 1) * BLK], op=ADD)
@@ -201,43 +212,45 @@ def tile_blockdiagmnistconvertible_pa_kernel(tc, x, W1, b1, Wb, bb, out):
             nc.vector.tensor_scalar_max(out=ot[n][:], in0=ot[n][:], scalar1=0.0)
             nc.sync.dma_start(out=out_rows[:, :, n * BLK:(n + 1) * BLK], in_=ot[n][:].rearrange("p (t o) -> p t o", t=4))
 
-        prep(0, "svsvss")
-        spread_bb(4, "s")
-        spread_bb(5, "s")
-        quant_w1(0)
-        quant_wb(0)
-        spread_bb(6, "v")
-        spread_bb(7, "v")
+        def finish_part(n, bt, eng):
+            part = ot[n][:, bt * BLK:(bt + 1) * BLK]
+            if eng == "v":
+                nc.vector.tensor_scalar_max(out=part, in0=part, scalar1=0.0)
+            else:
+                nc.scalar.activation(out=part, in_=part, func=RELU)
+            nc.sync.dma_start(out=out_rows[:, bt, n * BLK:(n + 1) * BLK], in_=part)
 
-        for i in range(NB + 1):
-            if i >= 1:
-                for bt in range(3):
-                    add_bias(i - 1, bt)
-            if i < NB:
-                stage1(i, 0)
-                stage1(i, 1)
-            if i >= 1:
-                stage2(i - 1, 3)
-                add_bias(i - 1, 3)
-                finish(i - 1)
-            if i < NB:
-                stage1(i, 2)
-                stage1(i, 3)
-            if i == 0:
-                prep(1, "ssssss")
-            elif i + 2 < NB:
-                prep(i + 2, "ssssss")
-            if i < NB:
-                regroup(i)
-                if i == 0:
-                    quant_h(i)
-                if i + 1 < NB:
-                    quant_w1(i + 1)
-                if i > 0:
-                    quant_h(i)
-                if i + 1 < NB:
-                    quant_wb(i + 1)
-                for bt in range(3):
-                    stage2(i, bt)
-            if i == 0:
-                prep(2, "ssssss")
+        def chunk(n):
+            return 0 <= n < NB
+
+        for p in range(-3, NB):
+            if chunk(p + 3):
+                prep_w1(p + 3, "svsv" if p + 3 < 2 else "ssss")
+            if chunk(p + 2):
+                prep_wb(p + 2)
+                for j in range(4):
+                    stage1(p + 2, j)
+            if p == -2:
+                spread_bb(2, "s")
+            if p == -1:
+                spread_bb(3, "s")
+            if chunk(p) and p < NB - 1:
+                for bt in range(4):
+                    add_bias(p, bt)
+            if chunk(p + 1):
+                regroup(p + 1)
+            if chunk(p) and p < NB - 1:
+                finish(p)
+            if p == NB - 1:
+                for bt in range(4):
+                    add_bias(p, bt)
+                    finish_part(p, bt, "v" if bt == 3 else "s")
+            if chunk(p + 1):
+                quant_h(p + 1)
+            if chunk(p + 3):
+                quant_w1(p + 3)
+            if chunk(p + 2):
+                quant_wb(p + 2)
+            if chunk(p + 1):
+                for bt in range(4):
+                    stage2(p + 1, bt)

@@ -9,7 +9,7 @@ U32 = mybir.dt.uint32
 U8 = mybir.dt.uint8
 FP8X4 = mybir.dt.float8_e4m3fn_x4
 RELU = mybir.ActivationFunctionType.Relu
-ADD = mybir.AluOpType.add
+ALU = mybir.AluOpType
 
 P = 128
 B = 512
@@ -18,6 +18,68 @@ HID = 4096
 BLK = 512
 NB = 8
 FLOPS = 2 * B * IN * HID + 2 * B * BLK * HID
+FLT_MAX = 3.4028234663852886e38
+
+LOADS = [("w", 0), ("w", 1), ("b", 0), ("w", 2), ("b", 1), ("w", 3), ("b", 2), ("w", 4), ("b", 3), ("w", 5), ("b", 4), ("w", 6), ("b", 5), ("w", 7), ("b", 6), ("b", 7)]
+ORDER = [
+    ("BM", 0), ("BE", 0, "v"), ("BM", 1), ("BE", 1, "s"), ("Tx", 0), ("Ex", 0, "s"),
+    ("Tx", 1), ("Ex", 1, "v"), ("Tx", 2), ("Ex", 2, "s"), ("Tx", 3), ("Ex", 3, "v"),
+    ("Qx", 0), ("Qx", 1), ("T1", 0, 0), ("E1", 0, 0, "s"), ("T1", 0, 1), ("E1", 0, 1, "v"),
+    ("T1", 0, 2), ("E1", 0, 2, "s"), ("T1", 0, 3), ("E1", 0, 3, "v"), ("QW", 0), ("T1", 1, 0),
+    ("E1", 1, 0, "s"), ("T1", 1, 1), ("E1", 1, 1, "v"), ("T1", 1, 2), ("E1", 1, 2, "s"), ("T1", 1, 3),
+    ("E1", 1, 3, "v"), ("TB", 0, 0), ("EB", 0, 0, "v"), ("TB", 0, 1), ("EB", 0, 1, "v"), ("M1", 0, 0),
+    ("H", 0, 0, "s"), ("M1", 0, 1), ("H", 0, 1, "s"), ("M1", 0, 2), ("H", 0, 2, "s"), ("M1", 0, 3),
+    ("H", 0, 3, "s"), ("QW", 1), ("QB", 0), ("T1", 2, 0), ("E1", 2, 0, "v"), ("T1", 2, 1),
+    ("E1", 2, 1, "s"), ("T1", 2, 2), ("E1", 2, 2, "v"), ("T1", 2, 3), ("E1", 2, 3, "s"), ("TB", 1, 0),
+    ("EB", 1, 0, "v"), ("TB", 1, 1), ("EB", 1, 1, "v"), ("M1", 1, 0), ("H", 1, 0, "s"), ("M1", 1, 1),
+    ("H", 1, 1, "s"), ("M1", 1, 2), ("H", 1, 2, "s"), ("M1", 1, 3), ("H", 1, 3, "s"), ("RG", 0),
+    ("QH", 0), ("QW", 2), ("QB", 1), ("T1", 3, 0), ("E1", 3, 0, "s"), ("T1", 3, 1),
+    ("E1", 3, 1, "s"), ("T1", 3, 2), ("E1", 3, 2, "s"), ("T1", 3, 3), ("E1", 3, 3, "s"), ("M2", 0, 0),
+    ("M2", 0, 1), ("M2", 0, 2), ("M2", 0, 3), ("TB", 2, 0), ("EB", 2, 0, "s"), ("TB", 2, 1),
+    ("EB", 2, 1, "s"), ("M1", 2, 0), ("H", 2, 0, "s"), ("M1", 2, 1), ("H", 2, 1, "s"), ("M1", 2, 2),
+    ("H", 2, 2, "s"), ("M1", 2, 3), ("H", 2, 3, "s"), ("RG", 1), ("A", 0, 0), ("RL", 0, 0, "g"),
+    ("ST", 0, 0), ("A", 0, 1), ("RL", 0, 1, "g"), ("ST", 0, 1), ("A", 0, 2), ("RL", 0, 2, "g"),
+    ("ST", 0, 2), ("A", 0, 3), ("RL", 0, 3, "v"), ("ST", 0, 3), ("QH", 1), ("QW", 3),
+    ("QB", 2), ("T1", 4, 0), ("E1", 4, 0, "s"), ("T1", 4, 1), ("E1", 4, 1, "s"), ("T1", 4, 2),
+    ("E1", 4, 2, "s"), ("T1", 4, 3), ("E1", 4, 3, "s"), ("M2", 1, 0), ("M2", 1, 1), ("M2", 1, 2),
+    ("M2", 1, 3), ("TB", 3, 0), ("EB", 3, 0, "s"), ("TB", 3, 1), ("EB", 3, 1, "s"), ("M1", 3, 0),
+    ("H", 3, 0, "s"), ("M1", 3, 1), ("H", 3, 1, "s"), ("M1", 3, 2), ("H", 3, 2, "s"), ("M1", 3, 3),
+    ("H", 3, 3, "s"), ("RG", 2), ("A", 1, 0), ("RL", 1, 0, "g"), ("ST", 1, 0), ("A", 1, 1),
+    ("RL", 1, 1, "g"), ("ST", 1, 1), ("A", 1, 2), ("RL", 1, 2, "g"), ("ST", 1, 2), ("A", 1, 3),
+    ("RL", 1, 3, "v"), ("ST", 1, 3), ("BM", 2), ("BE", 2, "s"), ("QH", 2), ("QW", 4),
+    ("QB", 3), ("T1", 5, 0), ("E1", 5, 0, "s"), ("T1", 5, 1), ("E1", 5, 1, "s"), ("T1", 5, 2),
+    ("E1", 5, 2, "s"), ("T1", 5, 3), ("E1", 5, 3, "s"), ("M2", 2, 0), ("M2", 2, 1), ("M2", 2, 2),
+    ("M2", 2, 3), ("TB", 4, 0), ("EB", 4, 0, "s"), ("TB", 4, 1), ("EB", 4, 1, "s"), ("M1", 4, 0),
+    ("H", 4, 0, "s"), ("M1", 4, 1), ("H", 4, 1, "s"), ("M1", 4, 2), ("H", 4, 2, "s"), ("M1", 4, 3),
+    ("H", 4, 3, "s"), ("RG", 3), ("A", 2, 0), ("RL", 2, 0, "g"), ("ST", 2, 0), ("A", 2, 1),
+    ("RL", 2, 1, "g"), ("ST", 2, 1), ("A", 2, 2), ("RL", 2, 2, "g"), ("ST", 2, 2), ("A", 2, 3),
+    ("RL", 2, 3, "v"), ("ST", 2, 3), ("BM", 3), ("BE", 3, "s"), ("QH", 3), ("QW", 5),
+    ("QB", 4), ("T1", 6, 0), ("E1", 6, 0, "s"), ("T1", 6, 1), ("E1", 6, 1, "s"), ("T1", 6, 2),
+    ("E1", 6, 2, "s"), ("T1", 6, 3), ("E1", 6, 3, "s"), ("M2", 3, 0), ("M2", 3, 1), ("M2", 3, 2),
+    ("M2", 3, 3), ("TB", 5, 0), ("EB", 5, 0, "s"), ("TB", 5, 1), ("EB", 5, 1, "s"), ("M1", 5, 0),
+    ("H", 5, 0, "s"), ("M1", 5, 1), ("H", 5, 1, "s"), ("M1", 5, 2), ("H", 5, 2, "s"), ("M1", 5, 3),
+    ("H", 5, 3, "s"), ("RG", 4), ("A", 3, 0), ("RL", 3, 0, "g"), ("ST", 3, 0), ("A", 3, 1),
+    ("RL", 3, 1, "g"), ("ST", 3, 1), ("A", 3, 2), ("RL", 3, 2, "g"), ("ST", 3, 2), ("A", 3, 3),
+    ("RL", 3, 3, "v"), ("ST", 3, 3), ("QH", 4), ("QW", 6), ("QB", 5), ("T1", 7, 0),
+    ("E1", 7, 0, "s"), ("T1", 7, 1), ("E1", 7, 1, "s"), ("T1", 7, 2), ("E1", 7, 2, "s"), ("T1", 7, 3),
+    ("E1", 7, 3, "s"), ("M2", 4, 0), ("M2", 4, 1), ("M2", 4, 2), ("M2", 4, 3), ("TB", 6, 0),
+    ("EB", 6, 0, "s"), ("TB", 6, 1), ("EB", 6, 1, "s"), ("M1", 6, 0), ("H", 6, 0, "s"), ("M1", 6, 1),
+    ("H", 6, 1, "s"), ("M1", 6, 2), ("H", 6, 2, "s"), ("M1", 6, 3), ("H", 6, 3, "s"), ("RG", 5),
+    ("A", 4, 0), ("RL", 4, 0, "g"), ("ST", 4, 0), ("A", 4, 1), ("RL", 4, 1, "g"), ("ST", 4, 1),
+    ("A", 4, 2), ("RL", 4, 2, "g"), ("ST", 4, 2), ("A", 4, 3), ("RL", 4, 3, "v"), ("ST", 4, 3),
+    ("QH", 5), ("QW", 7), ("QB", 6), ("M2", 5, 0), ("M2", 5, 1), ("M2", 5, 2),
+    ("M2", 5, 3), ("TB", 7, 0), ("EB", 7, 0, "s"), ("TB", 7, 1), ("EB", 7, 1, "s"), ("M1", 7, 0),
+    ("H", 7, 0, "s"), ("M1", 7, 1), ("H", 7, 1, "s"), ("M1", 7, 2), ("H", 7, 2, "s"), ("M1", 7, 3),
+    ("H", 7, 3, "s"), ("RG", 6), ("A", 5, 0), ("RL", 5, 0, "g"), ("ST", 5, 0), ("A", 5, 1),
+    ("RL", 5, 1, "g"), ("ST", 5, 1), ("A", 5, 2), ("RL", 5, 2, "g"), ("ST", 5, 2), ("A", 5, 3),
+    ("RL", 5, 3, "v"), ("ST", 5, 3), ("QH", 6), ("QB", 7), ("M2", 6, 0), ("M2", 6, 1),
+    ("M2", 6, 2), ("M2", 6, 3), ("RG", 7), ("A", 6, 0), ("RL", 6, 0, "g"), ("ST", 6, 0),
+    ("A", 6, 1), ("RL", 6, 1, "g"), ("ST", 6, 1), ("A", 6, 2), ("RL", 6, 2, "g"), ("ST", 6, 2),
+    ("A", 6, 3), ("RL", 6, 3, "v"), ("ST", 6, 3), ("QH", 7), ("M2", 7, 0), ("M2", 7, 1),
+    ("M2", 7, 2), ("M2", 7, 3), ("A", 7, 0), ("RL", 7, 0, "s"), ("ST", 7, 0), ("A", 7, 1),
+    ("RL", 7, 1, "s"), ("ST", 7, 1), ("A", 7, 2), ("RL", 7, 2, "s"), ("ST", 7, 2), ("A", 7, 3),
+    ("RL", 7, 3, "v"), ("ST", 7, 3),
+]
 
 
 def tile_blockdiagmnistconvertible_pa_kernel(tc, x, W1, b1, Wb, bb, out):
@@ -26,8 +88,7 @@ def tile_blockdiagmnistconvertible_pa_kernel(tc, x, W1, b1, Wb, bb, out):
         const = ctx.enter_context(tc.tile_pool(name="const", bufs=1))
         w1_pool = ctx.enter_context(tc.tile_pool(name="w1_pool", bufs=NB))
         wb_pool = ctx.enter_context(tc.tile_pool(name="wb_pool", bufs=NB))
-        two = ctx.enter_context(tc.tile_pool(name="two", bufs=2))
-        three = ctx.enter_context(tc.tile_pool(name="three", bufs=3))
+        work = ctx.enter_context(tc.tile_pool(name="work", bufs=2))
         ring_s = ctx.enter_context(tc.psum_pool(name="ring_s", bufs=4))
         ring_v = ctx.enter_context(tc.psum_pool(name="ring_v", bufs=4))
         ctx.enter_context(tc.manual_schedule())
@@ -49,28 +110,21 @@ def tile_blockdiagmnistconvertible_pa_kernel(tc, x, W1, b1, Wb, bb, out):
 
         w1_sbs = {}
         wb_sbs = {}
-
-        def load_w1(n):
-            w1_sb = w1_pool.tile([P, 4 * IN], BF16)
-            w1_sbs[n] = w1_sb
-            w1_rows = W1[n * BLK:(n + 1) * BLK, :].rearrange("(u p e) k -> p u e k", u=2, p=P, e=2)
-            w1_dst = w1_sb[:].rearrange("p (u e k) -> p u e k", u=2, e=2)
-            if n == 0:
-                for u in range(2):
-                    nc.sync.dma_start(out=w1_dst[:, u, :, :], in_=w1_rows[:, u, :, :])
+        for kind, n in LOADS:
+            if kind == "w":
+                w1_sb = w1_pool.tile([P, 4 * IN], BF16)
+                w1_sbs[n] = w1_sb
+                w1_rows = W1[n * BLK:(n + 1) * BLK, :].rearrange("(u p e) k -> p u e k", u=2, p=P, e=2)
+                w1_dst = w1_sb[:].rearrange("p (u e k) -> p u e k", u=2, e=2)
+                if n == 0:
+                    for u in range(2):
+                        nc.sync.dma_start(out=w1_dst[:, u, :, :], in_=w1_rows[:, u, :, :])
+                else:
+                    nc.sync.dma_start(out=w1_dst, in_=w1_rows)
             else:
-                nc.sync.dma_start(out=w1_dst, in_=w1_rows)
-
-        def load_wb(n):
-            wb_sb = wb_pool.tile([P, 4 * BLK], BF16)
-            wb_sbs[n] = wb_sb
-            nc.sync.dma_start(out=wb_sb[:].rearrange("p (j k) -> p j k", j=4), in_=Wb[n].rearrange("(p j) k -> p j k", j=4))
-
-        load_w1(0)
-        for n in range(1, NB):
-            load_w1(n)
-            load_wb(n - 1)
-        load_wb(NB - 1)
+                wb_sb = wb_pool.tile([P, 4 * BLK], BF16)
+                wb_sbs[n] = wb_sb
+                nc.sync.dma_start(out=wb_sb[:].rearrange("p (j k) -> p j k", j=4), in_=Wb[n].rearrange("(p j) k -> p j k", j=4))
 
         identb = const.tile([P, P], BF16)
         nc.vector.tensor_copy(out=identb[:], in_=ident[:])
@@ -96,30 +150,14 @@ def tile_blockdiagmnistconvertible_pa_kernel(tc, x, W1, b1, Wb, bb, out):
         nc.vector.tensor_copy(out=b1f[:], in_=b1p[:].bitcast(BF16))
 
         bbb = const.tile([P, HID], BF16)
-
-        def spread_bb(pair, eng):
-            wide = ring_v.tile([P, 2 * BLK], BF16, tag="acc")
-            for s in range(2):
-                n = 2 * pair + s
-                nc.tensor.matmul(out=wide[:, s * BLK:(s + 1) * BLK], lhsT=identb[:, n:n + 1].to_broadcast([P, P]), rhs=bbz[:],
-                                 start=True, stop=True)
-            copy_out(eng, bbb[:, 2 * pair * BLK:2 * (pair + 1) * BLK], wide[:])
-
-        spread_bb(0, "v")
-        spread_bb(1, "s")
-
         xg = const.tile([P, 4 * IN], BF16, align_bytes=64)
         xq = const.tile([P, IN], U32, align_bytes=64)
         xs = const.tile([P, IN], U8, align_bytes=64)
         x32 = x_sb[:].bitcast(F32)
         xg32 = xg[:].bitcast(F32).rearrange("p (g b c u) -> p g b c u", g=2, b=4, u=2)
-        for bt in range(4):
-            bank = transposes(x32, 512 * bt)
-            copy_out("sv"[bt % 2], xg32[:, :, bt, :, :], bank[:].rearrange("p (g u c) -> p g c u", g=2, u=2))
-        for g in range(2):
-            nc.vector.quantize_mx(out=xq[:, g * B:(g + 1) * B].bitcast(FP8X4), scales=xs[:, g * B:(g + 1) * B],
-                                  in_=xg[:, g * 4 * B:(g + 1) * 4 * B])
+        out_rows = out.rearrange("(c t) o -> c t o", t=4)
 
+        banks = {}
         w1g = {}
         wbg = {}
         w1q = {}
@@ -131,126 +169,111 @@ def tile_blockdiagmnistconvertible_pa_kernel(tc, x, W1, b1, Wb, bb, out):
         hq = {}
         hs = {}
         ot = {}
-        accs = {}
 
-        def prep_w1(n, engs):
-            w1g_t = two.tile([P, 4 * IN], BF16, align_bytes=64)
-            w1g[n] = w1g_t
-            w132 = w1_sbs[n][:].bitcast(F32)
-            g32 = w1g_t[:].bitcast(F32)
-            for j in range(4):
-                bank = transposes(w132, 512 * j)
-                copy_out(engs[j], g32[:, 512 * j:512 * (j + 1)].rearrange("p (g c u) -> p g c u", g=2, u=2),
-                         bank[:].rearrange("p (g u c) -> p g c u", g=2, u=2))
-
-        def prep_wb(n):
-            wbg_t = two.tile([P, 4 * BLK], BF16, align_bytes=64)
-            wbg[n] = wbg_t
-            wb32 = wb_sbs[n][:].bitcast(F32)
-            b32 = wbg_t[:].bitcast(F32).rearrange("p (c h q) -> p c h q", h=2, q=4)
-            for hb in range(2):
-                bank = transposes(wb32, 512 * hb)
-                copy_out("s", b32[:, :, hb, :], bank[:].rearrange("p (q c) -> p c q", q=4))
-
-        def quant_w1(n):
-            w1q_t = three.tile([P, IN], U32, align_bytes=64)
-            w1s_t = three.tile([P, IN], U8, align_bytes=64)
-            w1q[n] = w1q_t
-            w1s[n] = w1s_t
-            nc.vector.quantize_mx(out=w1q_t[:].bitcast(FP8X4), scales=w1s_t[:], in_=w1g[n][:])
-
-        def quant_wb(n):
-            wbq_t = three.tile([P, BLK], U32, align_bytes=64)
-            wbs_t = three.tile([P, BLK], U8, align_bytes=64)
-            wbq[n] = wbq_t
-            wbs[n] = wbs_t
-            nc.vector.quantize_mx(out=wbq_t[:].bitcast(FP8X4), scales=wbs_t[:], in_=wbg[n][:])
-
-        def stage1(n, j):
-            if j == 0:
-                hpl_t = three.tile([P, 4 * B], BF16)
-                hpl[n] = hpl_t
-            hp = ring_s.tile([P, B], F32, tag="bank")
-            for g in range(2):
-                lo = (2 * j + g) * P
-                nc.tensor.matmul_mx(out=hp[:], lhsT=w1q[n][:, lo:lo + P].bitcast(FP8X4), lhsT_scale=w1s[n][:, lo:lo + P],
-                                    rhs=xq[:, g * B:(g + 1) * B].bitcast(FP8X4), rhs_scale=xs[:, g * B:(g + 1) * B],
-                                    start=(g == 0), stop=(g == 1))
-            nc.scalar.activation(out=hpl[n][:, j * B:(j + 1) * B], in_=hp[:], func=RELU,
-                                 bias=b1f[:, 4 * n + j:4 * n + j + 1], scale=1.0)
-
-        def regroup(n):
-            hg_t = two.tile([P, 4 * B], BF16, align_bytes=64)
-            hg[n] = hg_t
-            nc.vector.tensor_copy(out=hg_t[:].rearrange("p (c i t) -> p c t i", i=4, t=4),
-                                  in_=hpl[n][:].rearrange("p (t c i) -> p c t i", t=4, i=4))
-
-        def quant_h(n):
-            hq_t = three.tile([P, B], U32, align_bytes=64)
-            hs_t = three.tile([P, B], U8, align_bytes=64)
-            hq[n] = hq_t
-            hs[n] = hs_t
-            nc.vector.quantize_mx(out=hq_t[:].bitcast(FP8X4), scales=hs_t[:], in_=hg[n][:])
-
-        def stage2(n, bt):
-            acc = ring_v.tile([P, BLK], F32)
-            accs[(n, bt)] = acc
-            nc.tensor.matmul_mx(out=acc[:], lhsT=hq[n][:, bt * P:(bt + 1) * P].bitcast(FP8X4),
-                                lhsT_scale=hs[n][:, bt * P:(bt + 1) * P],
-                                rhs=wbq[n][:].bitcast(FP8X4), rhs_scale=wbs[n][:], start=True, stop=True)
-
-        def add_bias(n, bt):
-            if bt == 0:
-                ot_t = three.tile([P, 4 * BLK], F32)
-                ot[n] = ot_t
-            nc.vector.tensor_tensor(out=ot[n][:, bt * BLK:(bt + 1) * BLK], in0=accs[(n, bt)][:],
-                                    in1=bbb[:, n * BLK:(n + 1) * BLK], op=ADD)
-
-        out_rows = out.rearrange("(c t) o -> c t o", t=4)
-
-        def finish(n):
-            nc.vector.tensor_scalar_max(out=ot[n][:], in0=ot[n][:], scalar1=0.0)
-            nc.sync.dma_start(out=out_rows[:, :, n * BLK:(n + 1) * BLK], in_=ot[n][:].rearrange("p (t o) -> p t o", t=4))
-
-        def finish_part(n, bt, eng):
-            part = ot[n][:, bt * BLK:(bt + 1) * BLK]
-            if eng == "v":
-                nc.vector.tensor_scalar_max(out=part, in0=part, scalar1=0.0)
-            else:
-                nc.scalar.activation(out=part, in_=part, func=RELU)
-            nc.sync.dma_start(out=out_rows[:, bt, n * BLK:(n + 1) * BLK], in_=part)
-
-        def chunk(n):
-            return 0 <= n < NB
-
-        for p in range(-3, NB):
-            if chunk(p + 3):
-                prep_w1(p + 3, "svsv" if p + 3 < 2 else "ssss")
-            if chunk(p + 2):
-                prep_wb(p + 2)
-                for j in range(4):
-                    stage1(p + 2, j)
-            if p == -2:
-                spread_bb(2, "s")
-            if p == -1:
-                spread_bb(3, "s")
-            if chunk(p) and p < NB - 1:
-                for bt in range(4):
-                    add_bias(p, bt)
-            if chunk(p + 1):
-                regroup(p + 1)
-            if chunk(p) and p < NB - 1:
-                finish(p)
-            if p == NB - 1:
-                for bt in range(4):
-                    add_bias(p, bt)
-                    finish_part(p, bt, "v" if bt == 3 else "s")
-            if chunk(p + 1):
-                quant_h(p + 1)
-            if chunk(p + 3):
-                quant_w1(p + 3)
-            if chunk(p + 2):
-                quant_wb(p + 2)
-            if chunk(p + 1):
-                for bt in range(4):
-                    stage2(p + 1, bt)
+        for op in ORDER:
+            f = op[0]
+            a = op[1]
+            if f == "BM":
+                wide = ring_v.tile([P, 2 * BLK], BF16, tag="acc")
+                banks[("bb", a)] = wide
+                for s in range(2):
+                    n = 2 * a + s
+                    nc.tensor.matmul(out=wide[:, s * BLK:(s + 1) * BLK], lhsT=identb[:, n:n + 1].to_broadcast([P, P]),
+                                     rhs=bbz[:], start=True, stop=True)
+            elif f == "BE":
+                copy_out(op[2], bbb[:, 2 * a * BLK:2 * (a + 1) * BLK], banks[("bb", a)][:])
+            elif f == "Tx":
+                banks[("x", a)] = transposes(x32, 512 * a)
+            elif f == "Ex":
+                copy_out(op[2], xg32[:, :, a, :, :], banks[("x", a)][:].rearrange("p (g u c) -> p g c u", g=2, u=2))
+            elif f == "Qx":
+                nc.vector.quantize_mx(out=xq[:, a * B:(a + 1) * B].bitcast(FP8X4), scales=xs[:, a * B:(a + 1) * B],
+                                      in_=xg[:, a * 4 * B:(a + 1) * 4 * B])
+            elif f == "T1":
+                banks[("w", a, op[2])] = transposes(w1_sbs[a][:].bitcast(F32), 512 * op[2])
+            elif f == "E1":
+                j = op[2]
+                if a not in w1g:
+                    w1g_t = work.tile([P, 4 * IN], BF16, align_bytes=64, bufs=2)
+                    w1g[a] = w1g_t
+                copy_out(op[3], w1g[a][:].bitcast(F32)[:, 512 * j:512 * (j + 1)].rearrange("p (g c u) -> p g c u", g=2, u=2),
+                         banks[("w", a, j)][:].rearrange("p (g u c) -> p g c u", g=2, u=2))
+            elif f == "QW":
+                w1q_t = work.tile([P, IN], U32, align_bytes=64, bufs=2)
+                w1s_t = work.tile([P, IN], U8, align_bytes=64, bufs=2)
+                w1q[a] = w1q_t
+                w1s[a] = w1s_t
+                nc.vector.quantize_mx(out=w1q_t[:].bitcast(FP8X4), scales=w1s_t[:], in_=w1g[a][:])
+            elif f == "TB":
+                banks[("b", a, op[2])] = transposes(wb_sbs[a][:].bitcast(F32), 512 * op[2])
+            elif f == "EB":
+                if a not in wbg:
+                    wbg_t = work.tile([P, 4 * BLK], BF16, align_bytes=64, bufs=2)
+                    wbg[a] = wbg_t
+                copy_out(op[3], wbg[a][:].bitcast(F32).rearrange("p (c h q) -> p c h q", h=2, q=4)[:, :, op[2], :],
+                         banks[("b", a, op[2])][:].rearrange("p (q c) -> p c q", q=4))
+            elif f == "QB":
+                wbq_t = work.tile([P, BLK], U32, align_bytes=64, bufs=3)
+                wbs_t = work.tile([P, BLK], U8, align_bytes=64, bufs=3)
+                wbq[a] = wbq_t
+                wbs[a] = wbs_t
+                nc.vector.quantize_mx(out=wbq_t[:].bitcast(FP8X4), scales=wbs_t[:], in_=wbg[a][:])
+            elif f == "M1":
+                j = op[2]
+                hp = ring_s.tile([P, B], F32, tag="bank")
+                banks[("h", a, j)] = hp
+                for g in range(2):
+                    lo = (2 * j + g) * P
+                    nc.tensor.matmul_mx(out=hp[:], lhsT=w1q[a][:, lo:lo + P].bitcast(FP8X4), lhsT_scale=w1s[a][:, lo:lo + P],
+                                        rhs=xq[:, g * B:(g + 1) * B].bitcast(FP8X4), rhs_scale=xs[:, g * B:(g + 1) * B],
+                                        start=(g == 0), stop=(g == 1))
+            elif f == "H":
+                j = op[2]
+                if a not in hpl:
+                    hpl_t = work.tile([P, 4 * B], BF16, bufs=2)
+                    hpl[a] = hpl_t
+                if op[3] == "v":
+                    nc.vector.tensor_scalar(out=hpl[a][:, j * B:(j + 1) * B], in0=banks[("h", a, j)][:],
+                                            scalar1=b1f[:, 4 * a + j:4 * a + j + 1], scalar2=0.0, op0=ALU.add, op1=ALU.max)
+                else:
+                    nc.scalar.activation(out=hpl[a][:, j * B:(j + 1) * B], in_=banks[("h", a, j)][:], func=RELU,
+                                         bias=b1f[:, 4 * a + j:4 * a + j + 1], scale=1.0)
+            elif f == "RG":
+                hg_t = work.tile([P, 4 * B], BF16, align_bytes=64, bufs=2)
+                hg[a] = hg_t
+                nc.vector.tensor_copy(out=hg_t[:].rearrange("p (c i t) -> p c t i", i=4, t=4),
+                                      in_=hpl[a][:].rearrange("p (t c i) -> p c t i", t=4, i=4))
+            elif f == "QH":
+                hq_t = work.tile([P, B], U32, align_bytes=64, bufs=2)
+                hs_t = work.tile([P, B], U8, align_bytes=64, bufs=2)
+                hq[a] = hq_t
+                hs[a] = hs_t
+                nc.vector.quantize_mx(out=hq_t[:].bitcast(FP8X4), scales=hs_t[:], in_=hg[a][:])
+            elif f == "M2":
+                bt = op[2]
+                acc = ring_v.tile([P, BLK], F32)
+                banks[("o", a, bt)] = acc
+                nc.tensor.matmul_mx(out=acc[:], lhsT=hq[a][:, bt * P:(bt + 1) * P].bitcast(FP8X4),
+                                    lhsT_scale=hs[a][:, bt * P:(bt + 1) * P],
+                                    rhs=wbq[a][:].bitcast(FP8X4), rhs_scale=wbs[a][:], start=True, stop=True)
+            elif f == "A":
+                bt = op[2]
+                if a not in ot:
+                    ot_t = work.tile([P, 4 * BLK], F32, bufs=3)
+                    ot[a] = ot_t
+                nc.vector.tensor_tensor(out=ot[a][:, bt * BLK:(bt + 1) * BLK], in0=banks[("o", a, bt)][:],
+                                        in1=bbb[:, a * BLK:(a + 1) * BLK], op=ALU.add)
+            elif f == "RL":
+                part = ot[a][:] if op[2] == "all" else ot[a][:, op[2] * BLK:(op[2] + 1) * BLK]
+                if op[3] == "v":
+                    nc.vector.tensor_scalar_max(out=part, in0=part, scalar1=0.0)
+                elif op[3] == "s":
+                    nc.scalar.activation(out=part, in_=part, func=RELU)
+                else:
+                    nc.gpsimd.tensor_scalar(out=part, in0=part, scalar1=FLT_MAX, scalar2=0.0, op0=ALU.min, op1=ALU.max)
+            elif f == "ST":
+                if op[2] == "all":
+                    nc.sync.dma_start(out=out_rows[:, :, a * BLK:(a + 1) * BLK], in_=ot[a][:].rearrange("p (t o) -> p t o", t=4))
+                else:
+                    bt = op[2]
+                    nc.sync.dma_start(out=out_rows[:, bt, a * BLK:(a + 1) * BLK], in_=ot[a][:, bt * BLK:(bt + 1) * BLK])

@@ -37,48 +37,48 @@ ORDER = [
     ("E1", 3, 1, "s"), ("T1", 3, 2), ("E1", 3, 2, "s"), ("T1", 3, 3), ("E1", 3, 3, "s"), ("M2", 0, 0),
     ("M2", 0, 1), ("M2", 0, 2), ("M2", 0, 3), ("TB", 2, 0), ("EB", 2, 0, "s"), ("TB", 2, 1),
     ("EB", 2, 1, "s"), ("M1", 2, 0), ("H", 2, 0, "s"), ("M1", 2, 1), ("H", 2, 1, "s"), ("M1", 2, 2),
-    ("H", 2, 2, "s"), ("M1", 2, 3), ("H", 2, 3, "s"), ("RG", 1), ("A", 0, 0), ("RL", 0, 0, "g"),
-    ("ST", 0, 0), ("A", 0, 1), ("RL", 0, 1, "g"), ("ST", 0, 1), ("A", 0, 2), ("RL", 0, 2, "g"),
+    ("H", 2, 2, "s"), ("M1", 2, 3), ("H", 2, 3, "s"), ("RG", 1), ("A", 0, 0), ("RL", 0, 0, "s"),
+    ("ST", 0, 0), ("A", 0, 1), ("RL", 0, 1, "v"), ("ST", 0, 1), ("A", 0, 2), ("RL", 0, 2, "v"),
     ("ST", 0, 2), ("A", 0, 3), ("RL", 0, 3, "v"), ("ST", 0, 3), ("QH", 1), ("QW", 3),
     ("QB", 2), ("T1", 4, 0), ("E1", 4, 0, "s"), ("T1", 4, 1), ("E1", 4, 1, "s"), ("T1", 4, 2),
     ("E1", 4, 2, "s"), ("T1", 4, 3), ("E1", 4, 3, "s"), ("M2", 1, 0), ("M2", 1, 1), ("M2", 1, 2),
     ("M2", 1, 3), ("TB", 3, 0), ("EB", 3, 0, "s"), ("TB", 3, 1), ("EB", 3, 1, "s"), ("M1", 3, 0),
     ("H", 3, 0, "s"), ("M1", 3, 1), ("H", 3, 1, "s"), ("M1", 3, 2), ("H", 3, 2, "s"), ("M1", 3, 3),
-    ("H", 3, 3, "s"), ("RG", 2), ("A", 1, 0), ("RL", 1, 0, "g"), ("ST", 1, 0), ("A", 1, 1),
-    ("RL", 1, 1, "g"), ("ST", 1, 1), ("A", 1, 2), ("RL", 1, 2, "g"), ("ST", 1, 2), ("A", 1, 3),
+    ("H", 3, 3, "s"), ("RG", 2), ("A", 1, 0), ("RL", 1, 0, "s"), ("ST", 1, 0), ("A", 1, 1),
+    ("RL", 1, 1, "v"), ("ST", 1, 1), ("A", 1, 2), ("RL", 1, 2, "v"), ("ST", 1, 2), ("A", 1, 3),
     ("RL", 1, 3, "v"), ("ST", 1, 3), ("BM", 2), ("BE", 2, "s"), ("QH", 2), ("QW", 4),
     ("QB", 3), ("T1", 5, 0), ("E1", 5, 0, "s"), ("T1", 5, 1), ("E1", 5, 1, "s"), ("T1", 5, 2),
     ("E1", 5, 2, "s"), ("T1", 5, 3), ("E1", 5, 3, "s"), ("M2", 2, 0), ("M2", 2, 1), ("M2", 2, 2),
     ("M2", 2, 3), ("TB", 4, 0), ("EB", 4, 0, "s"), ("TB", 4, 1), ("EB", 4, 1, "s"), ("M1", 4, 0),
     ("H", 4, 0, "s"), ("M1", 4, 1), ("H", 4, 1, "s"), ("M1", 4, 2), ("H", 4, 2, "s"), ("M1", 4, 3),
-    ("H", 4, 3, "s"), ("RG", 3), ("A", 2, 0), ("RL", 2, 0, "g"), ("ST", 2, 0), ("A", 2, 1),
-    ("RL", 2, 1, "g"), ("ST", 2, 1), ("A", 2, 2), ("RL", 2, 2, "g"), ("ST", 2, 2), ("A", 2, 3),
+    ("H", 4, 3, "s"), ("RG", 3), ("A", 2, 0), ("RL", 2, 0, "s"), ("ST", 2, 0), ("A", 2, 1),
+    ("RL", 2, 1, "v"), ("ST", 2, 1), ("A", 2, 2), ("RL", 2, 2, "v"), ("ST", 2, 2), ("A", 2, 3),
     ("RL", 2, 3, "v"), ("ST", 2, 3), ("BM", 3), ("BE", 3, "s"), ("QH", 3), ("QW", 5),
     ("QB", 4), ("T1", 6, 0), ("E1", 6, 0, "s"), ("T1", 6, 1), ("E1", 6, 1, "s"), ("T1", 6, 2),
     ("E1", 6, 2, "s"), ("T1", 6, 3), ("E1", 6, 3, "s"), ("M2", 3, 0), ("M2", 3, 1), ("M2", 3, 2),
     ("M2", 3, 3), ("TB", 5, 0), ("EB", 5, 0, "s"), ("TB", 5, 1), ("EB", 5, 1, "s"), ("M1", 5, 0),
     ("H", 5, 0, "s"), ("M1", 5, 1), ("H", 5, 1, "s"), ("M1", 5, 2), ("H", 5, 2, "s"), ("M1", 5, 3),
-    ("H", 5, 3, "s"), ("RG", 4), ("A", 3, 0), ("RL", 3, 0, "g"), ("ST", 3, 0), ("A", 3, 1),
-    ("RL", 3, 1, "g"), ("ST", 3, 1), ("A", 3, 2), ("RL", 3, 2, "g"), ("ST", 3, 2), ("A", 3, 3),
+    ("H", 5, 3, "s"), ("RG", 4), ("A", 3, 0), ("RL", 3, 0, "s"), ("ST", 3, 0), ("A", 3, 1),
+    ("RL", 3, 1, "s"), ("ST", 3, 1), ("A", 3, 2), ("RL", 3, 2, "v"), ("ST", 3, 2), ("A", 3, 3),
     ("RL", 3, 3, "v"), ("ST", 3, 3), ("QH", 4), ("QW", 6), ("QB", 5), ("T1", 7, 0),
     ("E1", 7, 0, "s"), ("T1", 7, 1), ("E1", 7, 1, "s"), ("T1", 7, 2), ("E1", 7, 2, "s"), ("T1", 7, 3),
     ("E1", 7, 3, "s"), ("M2", 4, 0), ("M2", 4, 1), ("M2", 4, 2), ("M2", 4, 3), ("TB", 6, 0),
     ("EB", 6, 0, "s"), ("TB", 6, 1), ("EB", 6, 1, "s"), ("M1", 6, 0), ("H", 6, 0, "s"), ("M1", 6, 1),
     ("H", 6, 1, "s"), ("M1", 6, 2), ("H", 6, 2, "s"), ("M1", 6, 3), ("H", 6, 3, "s"), ("RG", 5),
-    ("A", 4, 0), ("RL", 4, 0, "g"), ("ST", 4, 0), ("A", 4, 1), ("RL", 4, 1, "g"), ("ST", 4, 1),
-    ("A", 4, 2), ("RL", 4, 2, "g"), ("ST", 4, 2), ("A", 4, 3), ("RL", 4, 3, "v"), ("ST", 4, 3),
+    ("A", 4, 0), ("RL", 4, 0, "s"), ("ST", 4, 0), ("A", 4, 1), ("RL", 4, 1, "s"), ("ST", 4, 1),
+    ("A", 4, 2), ("RL", 4, 2, "v"), ("ST", 4, 2), ("A", 4, 3), ("RL", 4, 3, "v"), ("ST", 4, 3),
     ("QH", 5), ("QW", 7), ("QB", 6), ("M2", 5, 0), ("M2", 5, 1), ("M2", 5, 2),
     ("M2", 5, 3), ("TB", 7, 0), ("EB", 7, 0, "s"), ("TB", 7, 1), ("EB", 7, 1, "s"), ("M1", 7, 0),
     ("H", 7, 0, "s"), ("M1", 7, 1), ("H", 7, 1, "s"), ("M1", 7, 2), ("H", 7, 2, "s"), ("M1", 7, 3),
-    ("H", 7, 3, "s"), ("RG", 6), ("A", 5, 0), ("RL", 5, 0, "g"), ("ST", 5, 0), ("A", 5, 1),
-    ("RL", 5, 1, "g"), ("ST", 5, 1), ("A", 5, 2), ("RL", 5, 2, "g"), ("ST", 5, 2), ("A", 5, 3),
-    ("RL", 5, 3, "v"), ("ST", 5, 3), ("QH", 6), ("QB", 7), ("M2", 6, 0), ("M2", 6, 1),
-    ("M2", 6, 2), ("M2", 6, 3), ("RG", 7), ("A", 6, 0), ("RL", 6, 0, "g"), ("ST", 6, 0),
-    ("A", 6, 1), ("RL", 6, 1, "g"), ("ST", 6, 1), ("A", 6, 2), ("RL", 6, 2, "g"), ("ST", 6, 2),
-    ("A", 6, 3), ("RL", 6, 3, "v"), ("ST", 6, 3), ("QH", 7), ("M2", 7, 0), ("M2", 7, 1),
+    ("H", 7, 3, "s"), ("RG", 6), ("A", 5, 0), ("RL", 5, 0, "s"), ("ST", 5, 0), ("A", 5, 1),
+    ("RL", 5, 1, "s"), ("ST", 5, 1), ("A", 5, 2), ("RL", 5, 2, "s"), ("ST", 5, 2), ("A", 5, 3),
+    ("RL", 5, 3, "s"), ("ST", 5, 3), ("QH", 6), ("QB", 7), ("M2", 6, 0), ("M2", 6, 1),
+    ("M2", 6, 2), ("M2", 6, 3), ("RG", 7), ("A", 6, 0), ("RL", 6, 0, "s"), ("ST", 6, 0),
+    ("A", 6, 1), ("RL", 6, 1, "s"), ("ST", 6, 1), ("A", 6, 2), ("RL", 6, 2, "s"), ("ST", 6, 2),
+    ("A", 6, 3), ("RL", 6, 3, "s"), ("ST", 6, 3), ("QH", 7), ("M2", 7, 0), ("M2", 7, 1),
     ("M2", 7, 2), ("M2", 7, 3), ("A", 7, 0), ("RL", 7, 0, "s"), ("ST", 7, 0), ("A", 7, 1),
     ("RL", 7, 1, "s"), ("ST", 7, 1), ("A", 7, 2), ("RL", 7, 2, "s"), ("ST", 7, 2), ("A", 7, 3),
-    ("RL", 7, 3, "v"), ("ST", 7, 3),
+    ("RL", 7, 3, "s"), ("ST", 7, 3),
 ]
 
 

@@ -38,47 +38,43 @@ ORDER = [
     ("M2", 0, 1), ("M2", 0, 2), ("M2", 0, 3), ("TB", 2, 0), ("EB", 2, 0, "s"), ("TB", 2, 1),
     ("EB", 2, 1, "s"), ("M1", 2, 0), ("H", 2, 0, "s"), ("M1", 2, 1), ("H", 2, 1, "s"), ("M1", 2, 2),
     ("H", 2, 2, "s"), ("M1", 2, 3), ("H", 2, 3, "s"), ("RG", 1), ("A", 0, 0), ("RL", 0, 0, "s"),
-    ("ST", 0, 0), ("A", 0, 1), ("RL", 0, 1, "v"), ("ST", 0, 1), ("A", 0, 2), ("RL", 0, 2, "v"),
-    ("ST", 0, 2), ("A", 0, 3), ("RL", 0, 3, "v"), ("ST", 0, 3), ("QH", 1), ("QW", 3),
-    ("QB", 2), ("T1", 4, 0), ("E1", 4, 0, "s"), ("T1", 4, 1), ("E1", 4, 1, "s"), ("T1", 4, 2),
-    ("E1", 4, 2, "s"), ("T1", 4, 3), ("E1", 4, 3, "s"), ("M2", 1, 0), ("M2", 1, 1), ("M2", 1, 2),
-    ("M2", 1, 3), ("TB", 3, 0), ("EB", 3, 0, "s"), ("TB", 3, 1), ("EB", 3, 1, "s"), ("M1", 3, 0),
-    ("H", 3, 0, "s"), ("M1", 3, 1), ("H", 3, 1, "s"), ("M1", 3, 2), ("H", 3, 2, "s"), ("M1", 3, 3),
-    ("H", 3, 3, "s"), ("RG", 2), ("A", 1, 0), ("RL", 1, 0, "s"), ("ST", 1, 0), ("A", 1, 1),
-    ("RL", 1, 1, "v"), ("ST", 1, 1), ("A", 1, 2), ("RL", 1, 2, "v"), ("ST", 1, 2), ("A", 1, 3),
-    ("RL", 1, 3, "v"), ("ST", 1, 3), ("BM", 2), ("BE", 2, "s"), ("QH", 2), ("QW", 4),
-    ("QB", 3), ("T1", 5, 0), ("E1", 5, 0, "s"), ("T1", 5, 1), ("E1", 5, 1, "s"), ("T1", 5, 2),
-    ("E1", 5, 2, "s"), ("T1", 5, 3), ("E1", 5, 3, "s"), ("M2", 2, 0), ("M2", 2, 1), ("M2", 2, 2),
-    ("M2", 2, 3), ("TB", 4, 0), ("EB", 4, 0, "s"), ("TB", 4, 1), ("EB", 4, 1, "s"), ("M1", 4, 0),
-    ("H", 4, 0, "s"), ("M1", 4, 1), ("H", 4, 1, "s"), ("M1", 4, 2), ("H", 4, 2, "s"), ("M1", 4, 3),
-    ("H", 4, 3, "s"), ("RG", 3), ("A", 2, 0), ("RL", 2, 0, "s"), ("ST", 2, 0), ("A", 2, 1),
-    ("RL", 2, 1, "v"), ("ST", 2, 1), ("A", 2, 2), ("RL", 2, 2, "v"), ("ST", 2, 2), ("A", 2, 3),
-    ("RL", 2, 3, "v"), ("ST", 2, 3), ("BM", 3), ("BE", 3, "s"), ("QH", 3), ("QW", 5),
+    ("ST", 0, 0), ("A", 0, 1), ("QH", 1), ("A", 0, 2), ("A", 0, 3), ("RL", 0, "123", "v"),
+    ("ST", 0, "123"), ("QW", 3), ("QB", 2), ("T1", 4, 0), ("E1", 4, 0, "s"), ("T1", 4, 1),
+    ("E1", 4, 1, "s"), ("T1", 4, 2), ("E1", 4, 2, "s"), ("T1", 4, 3), ("E1", 4, 3, "s"), ("M2", 1, 0),
+    ("M2", 1, 1), ("M2", 1, 2), ("M2", 1, 3), ("TB", 3, 0), ("EB", 3, 0, "s"), ("TB", 3, 1),
+    ("EB", 3, 1, "s"), ("M1", 3, 0), ("H", 3, 0, "s"), ("M1", 3, 1), ("H", 3, 1, "s"), ("M1", 3, 2),
+    ("H", 3, 2, "s"), ("M1", 3, 3), ("H", 3, 3, "s"), ("RG", 2), ("A", 1, 0), ("RL", 1, 0, "s"),
+    ("ST", 1, 0), ("A", 1, 1), ("QH", 2), ("A", 1, 2), ("A", 1, 3), ("RL", 1, "123", "v"),
+    ("ST", 1, "123"), ("BM", 2), ("BE", 2, "s"), ("QW", 4), ("QB", 3), ("T1", 5, 0),
+    ("E1", 5, 0, "s"), ("T1", 5, 1), ("E1", 5, 1, "s"), ("T1", 5, 2), ("E1", 5, 2, "s"), ("T1", 5, 3),
+    ("E1", 5, 3, "s"), ("M2", 2, 0), ("M2", 2, 1), ("M2", 2, 2), ("M2", 2, 3), ("TB", 4, 0),
+    ("EB", 4, 0, "s"), ("TB", 4, 1), ("EB", 4, 1, "s"), ("M1", 4, 0), ("H", 4, 0, "s"), ("M1", 4, 1),
+    ("H", 4, 1, "s"), ("M1", 4, 2), ("H", 4, 2, "s"), ("M1", 4, 3), ("H", 4, 3, "s"), ("RG", 3),
+    ("A", 2, 0), ("RL", 2, 0, "s"), ("ST", 2, 0), ("A", 2, 1), ("QH", 3), ("A", 2, 2),
+    ("A", 2, 3), ("RL", 2, "123", "v"), ("ST", 2, "123"), ("BM", 3), ("BE", 3, "s"), ("QW", 5),
     ("QB", 4), ("T1", 6, 0), ("E1", 6, 0, "s"), ("T1", 6, 1), ("E1", 6, 1, "s"), ("T1", 6, 2),
     ("E1", 6, 2, "s"), ("T1", 6, 3), ("E1", 6, 3, "s"), ("M2", 3, 0), ("M2", 3, 1), ("M2", 3, 2),
     ("M2", 3, 3), ("TB", 5, 0), ("EB", 5, 0, "s"), ("TB", 5, 1), ("EB", 5, 1, "s"), ("M1", 5, 0),
     ("H", 5, 0, "s"), ("M1", 5, 1), ("H", 5, 1, "s"), ("M1", 5, 2), ("H", 5, 2, "s"), ("M1", 5, 3),
     ("H", 5, 3, "s"), ("RG", 4), ("A", 3, 0), ("RL", 3, 0, "s"), ("ST", 3, 0), ("A", 3, 1),
-    ("RL", 3, 1, "s"), ("ST", 3, 1), ("A", 3, 2), ("RL", 3, 2, "v"), ("ST", 3, 2), ("A", 3, 3),
-    ("RL", 3, 3, "v"), ("ST", 3, 3), ("QH", 4), ("QW", 6), ("QB", 5), ("T1", 7, 0),
-    ("E1", 7, 0, "s"), ("T1", 7, 1), ("E1", 7, 1, "s"), ("T1", 7, 2), ("E1", 7, 2, "s"), ("T1", 7, 3),
-    ("E1", 7, 3, "s"), ("M2", 4, 0), ("M2", 4, 1), ("M2", 4, 2), ("M2", 4, 3), ("TB", 6, 0),
-    ("EB", 6, 0, "s"), ("TB", 6, 1), ("EB", 6, 1, "s"), ("M1", 6, 0), ("H", 6, 0, "s"), ("M1", 6, 1),
-    ("H", 6, 1, "s"), ("M1", 6, 2), ("H", 6, 2, "s"), ("M1", 6, 3), ("H", 6, 3, "s"), ("RG", 5),
-    ("A", 4, 0), ("RL", 4, 0, "s"), ("ST", 4, 0), ("A", 4, 1), ("RL", 4, 1, "s"), ("ST", 4, 1),
-    ("A", 4, 2), ("RL", 4, 2, "v"), ("ST", 4, 2), ("A", 4, 3), ("RL", 4, 3, "v"), ("ST", 4, 3),
-    ("QH", 5), ("QW", 7), ("QB", 6), ("M2", 5, 0), ("M2", 5, 1), ("M2", 5, 2),
-    ("M2", 5, 3), ("TB", 7, 0), ("EB", 7, 0, "s"), ("TB", 7, 1), ("EB", 7, 1, "s"), ("M1", 7, 0),
-    ("H", 7, 0, "s"), ("M1", 7, 1), ("H", 7, 1, "s"), ("M1", 7, 2), ("H", 7, 2, "s"), ("M1", 7, 3),
-    ("H", 7, 3, "s"), ("RG", 6), ("A", 5, 0), ("RL", 5, 0, "s"), ("ST", 5, 0), ("A", 5, 1),
-    ("RL", 5, 1, "s"), ("ST", 5, 1), ("A", 5, 2), ("RL", 5, 2, "s"), ("ST", 5, 2), ("A", 5, 3),
-    ("RL", 5, 3, "s"), ("ST", 5, 3), ("QH", 6), ("QB", 7), ("M2", 6, 0), ("M2", 6, 1),
-    ("M2", 6, 2), ("M2", 6, 3), ("RG", 7), ("A", 6, 0), ("RL", 6, 0, "s"), ("ST", 6, 0),
-    ("A", 6, 1), ("RL", 6, 1, "s"), ("ST", 6, 1), ("A", 6, 2), ("RL", 6, 2, "s"), ("ST", 6, 2),
-    ("A", 6, 3), ("RL", 6, 3, "s"), ("ST", 6, 3), ("QH", 7), ("M2", 7, 0), ("M2", 7, 1),
-    ("M2", 7, 2), ("M2", 7, 3), ("A", 7, 0), ("RL", 7, 0, "s"), ("ST", 7, 0), ("A", 7, 1),
-    ("RL", 7, 1, "s"), ("ST", 7, 1), ("A", 7, 2), ("RL", 7, 2, "s"), ("ST", 7, 2), ("A", 7, 3),
-    ("RL", 7, 3, "s"), ("ST", 7, 3),
+    ("QH", 4), ("A", 3, 2), ("A", 3, 3), ("RL", 3, "123", "v"), ("ST", 3, "123"), ("QW", 6),
+    ("QB", 5), ("T1", 7, 0), ("E1", 7, 0, "s"), ("T1", 7, 1), ("E1", 7, 1, "s"), ("T1", 7, 2),
+    ("E1", 7, 2, "s"), ("T1", 7, 3), ("E1", 7, 3, "s"), ("M2", 4, 0), ("M2", 4, 1), ("M2", 4, 2),
+    ("M2", 4, 3), ("TB", 6, 0), ("EB", 6, 0, "s"), ("TB", 6, 1), ("EB", 6, 1, "s"), ("M1", 6, 0),
+    ("H", 6, 0, "s"), ("M1", 6, 1), ("H", 6, 1, "s"), ("M1", 6, 2), ("H", 6, 2, "s"), ("M1", 6, 3),
+    ("H", 6, 3, "s"), ("RG", 5), ("A", 4, 0), ("RL", 4, 0, "s"), ("ST", 4, 0), ("A", 4, 1),
+    ("QH", 5), ("A", 4, 2), ("A", 4, 3), ("RL", 4, "123", "v"), ("ST", 4, "123"), ("QW", 7),
+    ("QB", 6), ("M2", 5, 0), ("M2", 5, 1), ("M2", 5, 2), ("M2", 5, 3), ("TB", 7, 0),
+    ("EB", 7, 0, "s"), ("TB", 7, 1), ("EB", 7, 1, "s"), ("M1", 7, 0), ("H", 7, 0, "s"), ("M1", 7, 1),
+    ("H", 7, 1, "s"), ("M1", 7, 2), ("H", 7, 2, "s"), ("M1", 7, 3), ("H", 7, 3, "s"), ("RG", 6),
+    ("A", 5, 0), ("RL", 5, 0, "s"), ("ST", 5, 0), ("A", 5, 1), ("QH", 6), ("RL", 5, 1, "s"),
+    ("ST", 5, 1), ("A", 5, 2), ("RL", 5, 2, "s"), ("ST", 5, 2), ("A", 5, 3), ("RL", 5, 3, "s"),
+    ("ST", 5, 3), ("QB", 7), ("M2", 6, 0), ("M2", 6, 1), ("M2", 6, 2), ("M2", 6, 3),
+    ("RG", 7), ("A", 6, 0), ("RL", 6, 0, "s"), ("ST", 6, 0), ("A", 6, 1), ("QH", 7),
+    ("RL", 6, 1, "s"), ("ST", 6, 1), ("A", 6, 2), ("RL", 6, 2, "s"), ("ST", 6, 2), ("A", 6, 3),
+    ("RL", 6, 3, "s"), ("ST", 6, 3), ("M2", 7, 0), ("M2", 7, 1), ("M2", 7, 2), ("M2", 7, 3),
+    ("A", 7, 0), ("RL", 7, 0, "s"), ("ST", 7, 0), ("A", 7, 1), ("RL", 7, 1, "v"), ("ST", 7, 1),
+    ("A", 7, 2), ("RL", 7, 2, "v"), ("ST", 7, 2), ("A", 7, 3), ("RL", 7, 3, "v"), ("ST", 7, 3),
 ]
 
 
@@ -169,6 +165,13 @@ def tile_blockdiagmnistconvertible_pa_kernel(tc, x, W1, b1, Wb, bb, out):
         hq = {}
         hs = {}
         ot = {}
+
+        def quarters(q):
+            if q == "all":
+                return 0, 4
+            if isinstance(q, str):
+                return int(q[0]), int(q[-1]) + 1
+            return q, q + 1
 
         for op in ORDER:
             f = op[0]
@@ -264,7 +267,8 @@ def tile_blockdiagmnistconvertible_pa_kernel(tc, x, W1, b1, Wb, bb, out):
                 nc.vector.tensor_tensor(out=ot[a][:, bt * BLK:(bt + 1) * BLK], in0=banks[("o", a, bt)][:],
                                         in1=bbb[:, a * BLK:(a + 1) * BLK], op=ALU.add)
             elif f == "RL":
-                part = ot[a][:] if op[2] == "all" else ot[a][:, op[2] * BLK:(op[2] + 1) * BLK]
+                lo, hi = quarters(op[2])
+                part = ot[a][:, lo * BLK:hi * BLK]
                 if op[3] == "v":
                     nc.vector.tensor_scalar_max(out=part, in0=part, scalar1=0.0)
                 elif op[3] == "s":
@@ -272,8 +276,6 @@ def tile_blockdiagmnistconvertible_pa_kernel(tc, x, W1, b1, Wb, bb, out):
                 else:
                     nc.gpsimd.tensor_scalar(out=part, in0=part, scalar1=FLT_MAX, scalar2=0.0, op0=ALU.min, op1=ALU.max)
             elif f == "ST":
-                if op[2] == "all":
-                    nc.sync.dma_start(out=out_rows[:, :, a * BLK:(a + 1) * BLK], in_=ot[a][:].rearrange("p (t o) -> p t o", t=4))
-                else:
-                    bt = op[2]
-                    nc.sync.dma_start(out=out_rows[:, bt, a * BLK:(a + 1) * BLK], in_=ot[a][:, bt * BLK:(bt + 1) * BLK])
+                lo, hi = quarters(op[2])
+                nc.sync.dma_start(out=out_rows[:, lo:hi, a * BLK:(a + 1) * BLK],
+                                  in_=ot[a][:].rearrange("p (t o) -> p t o", t=4)[:, lo:hi, :])

@@ -34,38 +34,38 @@ ORDER = [
     ("EB", 1, 0, "v"), ("TB", 1, 1), ("EB", 1, 1, "v"), ("M1", 1, 0), ("H", 1, 0, "s"), ("M1", 1, 1),
     ("H", 1, 1, "s"), ("M1", 1, 2), ("H", 1, 2, "s"), ("M1", 1, 3), ("H", 1, 3, "s"), ("RG", 0),
     ("QH", 0), ("QW", 2), ("QB", 1), ("T1", 3, 0), ("E1", 3, 0, "s"), ("T1", 3, 1),
-    ("E1", 3, 1, "s"), ("T1", 3, 2), ("E1", 3, 2, "s"), ("T1", 3, 3), ("E1", 3, 3, "s"), ("M2", 0, 0),
-    ("M2", 0, 1), ("M2", 0, 2), ("M2", 0, 3), ("TB", 2, 0), ("EB", 2, 0, "s"), ("TB", 2, 1),
-    ("EB", 2, 1, "s"), ("M1", 2, 0), ("H", 2, 0, "s"), ("M1", 2, 1), ("H", 2, 1, "s"), ("M1", 2, 2),
+    ("E1", 3, 1, "s"), ("T1", 3, 2), ("E1", 3, 2, "s"), ("T1", 3, 3), ("E1", 3, 3, "s"), ("TB", 2, 0),
+    ("EB", 2, 0, "s"), ("TB", 2, 1), ("EB", 2, 1, "s"), ("M2", 0, 0), ("M2", 0, 1), ("M2", 0, 2),
+    ("M2", 0, 3), ("M1", 2, 0), ("H", 2, 0, "s"), ("M1", 2, 1), ("H", 2, 1, "s"), ("M1", 2, 2),
     ("H", 2, 2, "s"), ("M1", 2, 3), ("H", 2, 3, "s"), ("RG", 1), ("A", 0, 0), ("RL", 0, 0, "s"),
     ("ST", 0, 0), ("A", 0, 1), ("QH", 1), ("A", 0, 2), ("A", 0, 3), ("RL", 0, "123", "v"),
     ("ST", 0, "123"), ("QW", 3), ("QB", 2), ("T1", 4, 0), ("E1", 4, 0, "s"), ("T1", 4, 1),
-    ("E1", 4, 1, "s"), ("T1", 4, 2), ("E1", 4, 2, "s"), ("T1", 4, 3), ("E1", 4, 3, "s"), ("M2", 1, 0),
-    ("M2", 1, 1), ("M2", 1, 2), ("M2", 1, 3), ("TB", 3, 0), ("EB", 3, 0, "s"), ("TB", 3, 1),
-    ("EB", 3, 1, "s"), ("M1", 3, 0), ("H", 3, 0, "s"), ("M1", 3, 1), ("H", 3, 1, "s"), ("M1", 3, 2),
+    ("E1", 4, 1, "s"), ("T1", 4, 2), ("E1", 4, 2, "s"), ("T1", 4, 3), ("E1", 4, 3, "s"), ("TB", 3, 0),
+    ("EB", 3, 0, "s"), ("TB", 3, 1), ("EB", 3, 1, "s"), ("M2", 1, 0), ("M2", 1, 1), ("M2", 1, 2),
+    ("M2", 1, 3), ("M1", 3, 0), ("H", 3, 0, "s"), ("M1", 3, 1), ("H", 3, 1, "s"), ("M1", 3, 2),
     ("H", 3, 2, "s"), ("M1", 3, 3), ("H", 3, 3, "s"), ("RG", 2), ("A", 1, 0), ("RL", 1, 0, "s"),
     ("ST", 1, 0), ("A", 1, 1), ("QH", 2), ("A", 1, 2), ("A", 1, 3), ("RL", 1, "123", "v"),
     ("ST", 1, "123"), ("BM", 2), ("BE", 2, "s"), ("QW", 4), ("QB", 3), ("T1", 5, 0),
     ("E1", 5, 0, "s"), ("T1", 5, 1), ("E1", 5, 1, "s"), ("T1", 5, 2), ("E1", 5, 2, "s"), ("T1", 5, 3),
-    ("E1", 5, 3, "s"), ("M2", 2, 0), ("M2", 2, 1), ("M2", 2, 2), ("M2", 2, 3), ("TB", 4, 0),
-    ("EB", 4, 0, "s"), ("TB", 4, 1), ("EB", 4, 1, "s"), ("M1", 4, 0), ("H", 4, 0, "s"), ("M1", 4, 1),
+    ("E1", 5, 3, "s"), ("TB", 4, 0), ("EB", 4, 0, "s"), ("TB", 4, 1), ("EB", 4, 1, "s"), ("M2", 2, 0),
+    ("M2", 2, 1), ("M2", 2, 2), ("M2", 2, 3), ("M1", 4, 0), ("H", 4, 0, "s"), ("M1", 4, 1),
     ("H", 4, 1, "s"), ("M1", 4, 2), ("H", 4, 2, "s"), ("M1", 4, 3), ("H", 4, 3, "s"), ("RG", 3),
     ("A", 2, 0), ("RL", 2, 0, "s"), ("ST", 2, 0), ("A", 2, 1), ("QH", 3), ("A", 2, 2),
     ("A", 2, 3), ("RL", 2, "123", "v"), ("ST", 2, "123"), ("BM", 3), ("BE", 3, "s"), ("QW", 5),
     ("QB", 4), ("T1", 6, 0), ("E1", 6, 0, "s"), ("T1", 6, 1), ("E1", 6, 1, "s"), ("T1", 6, 2),
-    ("E1", 6, 2, "s"), ("T1", 6, 3), ("E1", 6, 3, "s"), ("M2", 3, 0), ("M2", 3, 1), ("M2", 3, 2),
-    ("M2", 3, 3), ("TB", 5, 0), ("EB", 5, 0, "s"), ("TB", 5, 1), ("EB", 5, 1, "s"), ("M1", 5, 0),
+    ("E1", 6, 2, "s"), ("T1", 6, 3), ("E1", 6, 3, "s"), ("TB", 5, 0), ("EB", 5, 0, "s"), ("TB", 5, 1),
+    ("EB", 5, 1, "s"), ("M2", 3, 0), ("M2", 3, 1), ("M2", 3, 2), ("M2", 3, 3), ("M1", 5, 0),
     ("H", 5, 0, "s"), ("M1", 5, 1), ("H", 5, 1, "s"), ("M1", 5, 2), ("H", 5, 2, "s"), ("M1", 5, 3),
     ("H", 5, 3, "s"), ("RG", 4), ("A", 3, 0), ("RL", 3, 0, "s"), ("ST", 3, 0), ("A", 3, 1),
     ("QH", 4), ("A", 3, 2), ("A", 3, 3), ("RL", 3, "123", "v"), ("ST", 3, "123"), ("QW", 6),
     ("QB", 5), ("T1", 7, 0), ("E1", 7, 0, "s"), ("T1", 7, 1), ("E1", 7, 1, "s"), ("T1", 7, 2),
-    ("E1", 7, 2, "s"), ("T1", 7, 3), ("E1", 7, 3, "s"), ("M2", 4, 0), ("M2", 4, 1), ("M2", 4, 2),
-    ("M2", 4, 3), ("TB", 6, 0), ("EB", 6, 0, "s"), ("TB", 6, 1), ("EB", 6, 1, "s"), ("M1", 6, 0),
+    ("E1", 7, 2, "s"), ("T1", 7, 3), ("E1", 7, 3, "s"), ("TB", 6, 0), ("EB", 6, 0, "s"), ("TB", 6, 1),
+    ("EB", 6, 1, "s"), ("M2", 4, 0), ("M2", 4, 1), ("M2", 4, 2), ("M2", 4, 3), ("M1", 6, 0),
     ("H", 6, 0, "s"), ("M1", 6, 1), ("H", 6, 1, "s"), ("M1", 6, 2), ("H", 6, 2, "s"), ("M1", 6, 3),
     ("H", 6, 3, "s"), ("RG", 5), ("A", 4, 0), ("RL", 4, 0, "s"), ("ST", 4, 0), ("A", 4, 1),
     ("QH", 5), ("A", 4, 2), ("A", 4, 3), ("RL", 4, "123", "v"), ("ST", 4, "123"), ("QW", 7),
-    ("QB", 6), ("M2", 5, 0), ("M2", 5, 1), ("M2", 5, 2), ("M2", 5, 3), ("TB", 7, 0),
-    ("EB", 7, 0, "s"), ("TB", 7, 1), ("EB", 7, 1, "s"), ("M1", 7, 0), ("H", 7, 0, "s"), ("M1", 7, 1),
+    ("QB", 6), ("TB", 7, 0), ("EB", 7, 0, "s"), ("TB", 7, 1), ("EB", 7, 1, "s"), ("M2", 5, 0),
+    ("M2", 5, 1), ("M2", 5, 2), ("M2", 5, 3), ("M1", 7, 0), ("H", 7, 0, "s"), ("M1", 7, 1),
     ("H", 7, 1, "s"), ("M1", 7, 2), ("H", 7, 2, "s"), ("M1", 7, 3), ("H", 7, 3, "s"), ("RG", 6),
     ("A", 5, 0), ("RL", 5, 0, "s"), ("ST", 5, 0), ("A", 5, 1), ("QH", 6), ("RL", 5, 1, "s"),
     ("ST", 5, 1), ("A", 5, 2), ("RL", 5, 2, "s"), ("ST", 5, 2), ("A", 5, 3), ("RL", 5, 3, "s"),
@@ -85,8 +85,8 @@ def tile_blockdiagmnistconvertible_pa_kernel(tc, x, W1, b1, Wb, bb, out):
         w1_pool = ctx.enter_context(tc.tile_pool(name="w1_pool", bufs=NB))
         wb_pool = ctx.enter_context(tc.tile_pool(name="wb_pool", bufs=NB))
         work = ctx.enter_context(tc.tile_pool(name="work", bufs=2))
-        ring_s = ctx.enter_context(tc.psum_pool(name="ring_s", bufs=4))
-        ring_v = ctx.enter_context(tc.psum_pool(name="ring_v", bufs=4))
+        ring_s = ctx.enter_context(tc.psum_pool(name="ring_s", bufs=8))
+        ring_v = ring_s
         ctx.enter_context(tc.manual_schedule())
 
         ident = const.tile([P, P], F32)
@@ -177,7 +177,7 @@ def tile_blockdiagmnistconvertible_pa_kernel(tc, x, W1, b1, Wb, bb, out):
             f = op[0]
             a = op[1]
             if f == "BM":
-                wide = ring_v.tile([P, 2 * BLK], BF16, tag="acc")
+                wide = ring_v.tile([P, 2 * BLK], BF16, tag="bank")
                 banks[("bb", a)] = wide
                 for s in range(2):
                     n = 2 * a + s
@@ -254,7 +254,7 @@ def tile_blockdiagmnistconvertible_pa_kernel(tc, x, W1, b1, Wb, bb, out):
                 nc.vector.quantize_mx(out=hq_t[:].bitcast(FP8X4), scales=hs_t[:], in_=hg[a][:])
             elif f == "M2":
                 bt = op[2]
-                acc = ring_v.tile([P, BLK], F32)
+                acc = ring_v.tile([P, BLK], F32, tag="bank")
                 banks[("o", a, bt)] = acc
                 nc.tensor.matmul_mx(out=acc[:], lhsT=hq[a][:, bt * P:(bt + 1) * P].bitcast(FP8X4),
                                     lhsT_scale=hs[a][:, bt * P:(bt + 1) * P],

@@ -9,273 +9,255 @@ U32 = mybir.dt.uint32
 U8 = mybir.dt.uint8
 FP8X4 = mybir.dt.float8_e4m3fn_x4
 RELU = mybir.ActivationFunctionType.Relu
-ALU = mybir.AluOpType
+ADD = mybir.AluOpType.add
 
 P = 128
-B = 512
-IN = 1024
+BATCH = 512
+K1 = 1024
 HID = 4096
-BLK = 512
-NB = 8
-FLOPS = 2 * B * IN * HID + 2 * B * BLK * HID
-FLT_MAX = 3.4028234663852886e38
+CHUNK = 512
+N_CHUNKS = HID // CHUNK
+TILES = 4
+BANK = 512
+PSUM_BANKS = 8
+W1_AHEAD = 3
+WB_AHEAD = 2
+STAGE1_AHEAD = 2
+HELPED = 2
+SCALAR_RELU = (5, 6)
 
-LOADS = [("w", 0), ("w", 1), ("b", 0), ("w", 2), ("b", 1), ("w", 3), ("b", 2), ("w", 4), ("b", 3), ("w", 5), ("b", 4), ("w", 6), ("b", 5), ("w", 7), ("b", 6), ("b", 7)]
-ORDER = [
-    ("BM", 0), ("BE", 0, "v"), ("BM", 1), ("BE", 1, "s"), ("Tx", 0), ("Ex", 0, "s"),
-    ("Tx", 1), ("Ex", 1, "v"), ("Tx", 2), ("Ex", 2, "s"), ("Tx", 3), ("Ex", 3, "v"),
-    ("Qx", 0), ("Qx", 1), ("T1", 0, 0), ("E1", 0, 0, "s"), ("T1", 0, 1), ("E1", 0, 1, "v"),
-    ("T1", 0, 2), ("E1", 0, 2, "s"), ("T1", 0, 3), ("E1", 0, 3, "v"), ("QW", 0), ("T1", 1, 0),
-    ("E1", 1, 0, "s"), ("T1", 1, 1), ("E1", 1, 1, "v"), ("T1", 1, 2), ("E1", 1, 2, "s"), ("T1", 1, 3),
-    ("E1", 1, 3, "v"), ("TB", 0, 0), ("EB", 0, 0, "v"), ("TB", 0, 1), ("EB", 0, 1, "v"), ("M1", 0, 0),
-    ("H", 0, 0, "s"), ("M1", 0, 1), ("H", 0, 1, "s"), ("M1", 0, 2), ("H", 0, 2, "s"), ("M1", 0, 3),
-    ("H", 0, 3, "s"), ("QW", 1), ("QB", 0), ("T1", 2, 0), ("E1", 2, 0, "v"), ("T1", 2, 1),
-    ("E1", 2, 1, "s"), ("T1", 2, 2), ("E1", 2, 2, "v"), ("T1", 2, 3), ("E1", 2, 3, "s"), ("TB", 1, 0),
-    ("EB", 1, 0, "v"), ("TB", 1, 1), ("EB", 1, 1, "v"), ("M1", 1, 0), ("H", 1, 0, "s"), ("M1", 1, 1),
-    ("H", 1, 1, "s"), ("M1", 1, 2), ("H", 1, 2, "s"), ("M1", 1, 3), ("H", 1, 3, "s"), ("RG", 0),
-    ("QH", 0), ("QW", 2), ("QB", 1), ("T1", 3, 0), ("E1", 3, 0, "s"), ("T1", 3, 1),
-    ("E1", 3, 1, "s"), ("T1", 3, 2), ("E1", 3, 2, "s"), ("T1", 3, 3), ("E1", 3, 3, "s"), ("TB", 2, 0),
-    ("EB", 2, 0, "s"), ("TB", 2, 1), ("EB", 2, 1, "s"), ("M2", 0, 0), ("M2", 0, 1), ("M2", 0, 2),
-    ("M2", 0, 3), ("M1", 2, 0), ("H", 2, 0, "s"), ("M1", 2, 1), ("H", 2, 1, "s"), ("M1", 2, 2),
-    ("H", 2, 2, "s"), ("M1", 2, 3), ("H", 2, 3, "s"), ("RG", 1), ("A", 0, 0), ("RL", 0, 0, "s"),
-    ("ST", 0, 0), ("A", 0, 1), ("QH", 1), ("A", 0, 2), ("A", 0, 3), ("RL", 0, "123", "v"),
-    ("ST", 0, "123"), ("QW", 3), ("QB", 2), ("T1", 4, 0), ("E1", 4, 0, "s"), ("T1", 4, 1),
-    ("E1", 4, 1, "s"), ("T1", 4, 2), ("E1", 4, 2, "s"), ("T1", 4, 3), ("E1", 4, 3, "s"), ("TB", 3, 0),
-    ("EB", 3, 0, "s"), ("TB", 3, 1), ("EB", 3, 1, "s"), ("M2", 1, 0), ("M2", 1, 1), ("M2", 1, 2),
-    ("M2", 1, 3), ("M1", 3, 0), ("H", 3, 0, "s"), ("M1", 3, 1), ("H", 3, 1, "s"), ("M1", 3, 2),
-    ("H", 3, 2, "s"), ("M1", 3, 3), ("H", 3, 3, "s"), ("RG", 2), ("A", 1, 0), ("RL", 1, 0, "s"),
-    ("ST", 1, 0), ("A", 1, 1), ("QH", 2), ("A", 1, 2), ("A", 1, 3), ("RL", 1, "123", "v"),
-    ("ST", 1, "123"), ("BM", 2), ("BE", 2, "s"), ("QW", 4), ("QB", 3), ("T1", 5, 0),
-    ("E1", 5, 0, "s"), ("T1", 5, 1), ("E1", 5, 1, "s"), ("T1", 5, 2), ("E1", 5, 2, "s"), ("T1", 5, 3),
-    ("E1", 5, 3, "s"), ("TB", 4, 0), ("EB", 4, 0, "s"), ("TB", 4, 1), ("EB", 4, 1, "s"), ("M2", 2, 0),
-    ("M2", 2, 1), ("M2", 2, 2), ("M2", 2, 3), ("M1", 4, 0), ("H", 4, 0, "s"), ("M1", 4, 1),
-    ("H", 4, 1, "s"), ("M1", 4, 2), ("H", 4, 2, "s"), ("M1", 4, 3), ("H", 4, 3, "s"), ("RG", 3),
-    ("A", 2, 0), ("RL", 2, 0, "s"), ("ST", 2, 0), ("A", 2, 1), ("QH", 3), ("A", 2, 2),
-    ("A", 2, 3), ("RL", 2, "123", "v"), ("ST", 2, "123"), ("BM", 3), ("BE", 3, "s"), ("QW", 5),
-    ("QB", 4), ("T1", 6, 0), ("E1", 6, 0, "s"), ("T1", 6, 1), ("E1", 6, 1, "s"), ("T1", 6, 2),
-    ("E1", 6, 2, "s"), ("T1", 6, 3), ("E1", 6, 3, "s"), ("TB", 5, 0), ("EB", 5, 0, "s"), ("TB", 5, 1),
-    ("EB", 5, 1, "s"), ("M2", 3, 0), ("M2", 3, 1), ("M2", 3, 2), ("M2", 3, 3), ("M1", 5, 0),
-    ("H", 5, 0, "s"), ("M1", 5, 1), ("H", 5, 1, "s"), ("M1", 5, 2), ("H", 5, 2, "s"), ("M1", 5, 3),
-    ("H", 5, 3, "s"), ("RG", 4), ("A", 3, 0), ("RL", 3, 0, "s"), ("ST", 3, 0), ("A", 3, 1),
-    ("QH", 4), ("A", 3, 2), ("A", 3, 3), ("RL", 3, "123", "v"), ("ST", 3, "123"), ("QW", 6),
-    ("QB", 5), ("T1", 7, 0), ("E1", 7, 0, "s"), ("T1", 7, 1), ("E1", 7, 1, "s"), ("T1", 7, 2),
-    ("E1", 7, 2, "s"), ("T1", 7, 3), ("E1", 7, 3, "s"), ("TB", 6, 0), ("EB", 6, 0, "s"), ("TB", 6, 1),
-    ("EB", 6, 1, "s"), ("M2", 4, 0), ("M2", 4, 1), ("M2", 4, 2), ("M2", 4, 3), ("M1", 6, 0),
-    ("H", 6, 0, "s"), ("M1", 6, 1), ("H", 6, 1, "s"), ("M1", 6, 2), ("H", 6, 2, "s"), ("M1", 6, 3),
-    ("H", 6, 3, "s"), ("RG", 5), ("A", 4, 0), ("RL", 4, 0, "s"), ("ST", 4, 0), ("A", 4, 1),
-    ("QH", 5), ("A", 4, 2), ("A", 4, 3), ("RL", 4, "123", "v"), ("ST", 4, "123"), ("QW", 7),
-    ("QB", 6), ("TB", 7, 0), ("EB", 7, 0, "s"), ("TB", 7, 1), ("EB", 7, 1, "s"), ("M2", 5, 0),
-    ("M2", 5, 1), ("M2", 5, 2), ("M2", 5, 3), ("M1", 7, 0), ("H", 7, 0, "s"), ("M1", 7, 1),
-    ("H", 7, 1, "s"), ("M1", 7, 2), ("H", 7, 2, "s"), ("M1", 7, 3), ("H", 7, 3, "s"), ("RG", 6),
-    ("A", 5, 0), ("RL", 5, 0, "s"), ("ST", 5, 0), ("A", 5, 1), ("QH", 6), ("RL", 5, 1, "s"),
-    ("ST", 5, 1), ("A", 5, 2), ("RL", 5, 2, "s"), ("ST", 5, 2), ("A", 5, 3), ("RL", 5, 3, "s"),
-    ("ST", 5, 3), ("QB", 7), ("M2", 6, 0), ("M2", 6, 1), ("M2", 6, 2), ("M2", 6, 3),
-    ("RG", 7), ("A", 6, 0), ("RL", 6, 0, "s"), ("ST", 6, 0), ("A", 6, 1), ("QH", 7),
-    ("RL", 6, 1, "s"), ("ST", 6, 1), ("A", 6, 2), ("RL", 6, 2, "s"), ("ST", 6, 2), ("A", 6, 3),
-    ("RL", 6, 3, "s"), ("ST", 6, 3), ("M2", 7, 0), ("M2", 7, 1), ("M2", 7, 2), ("M2", 7, 3),
-    ("A", 7, 0), ("RL", 7, 0, "s"), ("ST", 7, 0), ("A", 7, 1), ("RL", 7, 1, "v"), ("ST", 7, 1),
-    ("A", 7, 2), ("RL", 7, 2, "v"), ("ST", 7, 2), ("A", 7, 3), ("RL", 7, 3, "v"), ("ST", 7, 3),
-]
+FLOPS = 2 * BATCH * K1 * HID + 2 * BATCH * CHUNK * HID
 
 
 def tile_blockdiagmnistconvertible_pa_kernel(tc, x, W1, b1, Wb, bb, out):
     nc = tc.nc
     with ExitStack() as ctx:
         const = ctx.enter_context(tc.tile_pool(name="const", bufs=1))
-        w1_pool = ctx.enter_context(tc.tile_pool(name="w1_pool", bufs=NB))
-        wb_pool = ctx.enter_context(tc.tile_pool(name="wb_pool", bufs=NB))
+        w1_pool = ctx.enter_context(tc.tile_pool(name="w1_pool", bufs=N_CHUNKS))
+        wb_pool = ctx.enter_context(tc.tile_pool(name="wb_pool", bufs=N_CHUNKS))
         work = ctx.enter_context(tc.tile_pool(name="work", bufs=2))
-        ring_s = ctx.enter_context(tc.psum_pool(name="ring_s", bufs=8))
-        ring_v = ring_s
+        slow = ctx.enter_context(tc.tile_pool(name="slow", bufs=3))
+        psum = ctx.enter_context(tc.psum_pool(name="psum", bufs=PSUM_BANKS))
         ctx.enter_context(tc.manual_schedule())
 
         ident = const.tile([P, P], F32)
         make_identity(nc, ident[:])
-        b1w = const.tile([P, 2 * P], BF16)
-        nc.vector.memset(b1w[:], 0.0)
-        bbz = const.tile([P, BLK], BF16)
-        nc.vector.memset(bbz[:], 0.0)
-        nc.sync.dma_start(out=b1w[0:16, :], in_=b1.rearrange("(r w) -> r w", w=2 * P))
-        nc.sync.dma_start(out=bbz[0:NB, :], in_=bb.rearrange("(n o) -> n o", o=BLK))
+        b1_rows = const.tile([P, 2 * P], BF16)
+        nc.vector.memset(b1_rows[:], 0.0)
+        bb_rows = const.tile([P, CHUNK], BF16)
+        nc.vector.memset(bb_rows[:], 0.0)
+        nc.sync.dma_start(out=b1_rows[0:2 * N_CHUNKS, :], in_=b1.rearrange("(r w) -> r w", w=2 * P))
+        nc.sync.dma_start(out=bb_rows[0:N_CHUNKS, :], in_=bb.rearrange("(n o) -> n o", o=CHUNK))
 
-        x_sb = const.tile([P, 4 * IN], BF16)
-        x_rows = x.rearrange("(p t) k -> p t k", t=4)
-        x_dst = x_sb[:].rearrange("p (t k) -> p t k", t=4)
+        x_sb = const.tile([P, TILES * K1], BF16)
+        x_src = x.rearrange("(c b) k -> c b k", b=TILES)
+        x_dst = x_sb[:].rearrange("c (b k) -> c b k", b=TILES)
         for half in range(2):
-            nc.sync.dma_start(out=x_dst[:, 2 * half:2 * half + 2, :], in_=x_rows[:, 2 * half:2 * half + 2, :])
+            nc.sync.dma_start(out=x_dst[:, 2 * half:2 * half + 2, :], in_=x_src[:, 2 * half:2 * half + 2, :])
 
-        w1_sbs = {}
-        wb_sbs = {}
-        for kind, n in LOADS:
-            if kind == "w":
-                w1_sb = w1_pool.tile([P, 4 * IN], BF16)
-                w1_sbs[n] = w1_sb
-                w1_rows = W1[n * BLK:(n + 1) * BLK, :].rearrange("(u p e) k -> p u e k", u=2, p=P, e=2)
-                w1_dst = w1_sb[:].rearrange("p (u e k) -> p u e k", u=2, e=2)
-                if n == 0:
-                    for u in range(2):
-                        nc.sync.dma_start(out=w1_dst[:, u, :, :], in_=w1_rows[:, u, :, :])
-                else:
-                    nc.sync.dma_start(out=w1_dst, in_=w1_rows)
+        w1_sb = {}
+        wb_sb = {}
+
+        def load_w1(n):
+            w1_tile = w1_pool.tile([P, TILES * K1], BF16)
+            w1_sb[n] = w1_tile
+            src = W1[n * CHUNK:(n + 1) * CHUNK, :].rearrange("(u p e) k -> p u e k", u=2, p=P, e=2)
+            dst = w1_tile[:].rearrange("p (u e k) -> p u e k", u=2, e=2)
+            if n == 0:
+                for u in range(2):
+                    nc.sync.dma_start(out=dst[:, u, :, :], in_=src[:, u, :, :])
             else:
-                wb_sb = wb_pool.tile([P, 4 * BLK], BF16)
-                wb_sbs[n] = wb_sb
-                nc.sync.dma_start(out=wb_sb[:].rearrange("p (j k) -> p j k", j=4), in_=Wb[n].rearrange("(p j) k -> p j k", j=4))
+                nc.sync.dma_start(out=dst, in_=src)
 
-        identb = const.tile([P, P], BF16)
-        nc.vector.tensor_copy(out=identb[:], in_=ident[:])
+        def load_wb(n):
+            wb_tile = wb_pool.tile([P, TILES * CHUNK], BF16)
+            wb_sb[n] = wb_tile
+            nc.sync.dma_start(out=wb_tile[:].rearrange("c (j k) -> c j k", j=TILES),
+                              in_=Wb[n].rearrange("(c j) k -> c j k", j=TILES))
 
-        def copy_out(eng, dst, src):
-            if eng == "v":
+        load_w1(0)
+        for n in range(1, N_CHUNKS):
+            load_w1(n)
+            load_wb(n - 1)
+        load_wb(N_CHUNKS - 1)
+
+        ident_bf = const.tile([P, P], BF16)
+        nc.vector.tensor_copy(out=ident_bf[:], in_=ident[:])
+
+        def copy_out(on_vector, dst, src):
+            if on_vector:
                 nc.vector.tensor_copy(out=dst, in_=src)
             else:
                 nc.scalar.copy(out=dst, in_=src)
 
-        def transposes(src32, first_word):
-            bank = ring_s.tile([P, 512], F32)
-            for q in range(4):
-                lo = first_word + P * q
-                nc.tensor.transpose(out=bank[:, P * q:P * (q + 1)], in_=src32[:, lo:lo + P], identity=ident[:])
+        def transpose_words(words, first):
+            bank = psum.tile([P, BANK], F32, tag="bank")
+            for i in range(4):
+                lo = first + P * i
+                nc.tensor.transpose(out=bank[:, P * i:P * (i + 1)], in_=words[:, lo:lo + P], identity=ident[:])
             return bank
 
-        b1bank = ring_s.tile([P, 512], F32, tag="bank")
-        nc.tensor.transpose(out=b1bank[:, 0:P], in_=b1w[:].bitcast(F32), identity=ident[:])
-        b1p = const.tile([P, 16], F32)
-        nc.vector.tensor_copy(out=b1p[:], in_=b1bank[:, 0:16])
-        b1f = const.tile([P, 32], F32)
-        nc.vector.tensor_copy(out=b1f[:], in_=b1p[:].bitcast(BF16))
+        b1_bank = psum.tile([P, BANK], F32, tag="bank")
+        nc.tensor.transpose(out=b1_bank[:, 0:P], in_=b1_rows[:].bitcast(F32), identity=ident[:])
+        b1_words = const.tile([P, 2 * N_CHUNKS], F32)
+        nc.vector.tensor_copy(out=b1_words[:], in_=b1_bank[:, 0:2 * N_CHUNKS])
+        b1_col = const.tile([P, TILES * N_CHUNKS], F32)
+        nc.vector.tensor_copy(out=b1_col[:], in_=b1_words[:].bitcast(BF16))
 
-        bbb = const.tile([P, HID], BF16)
-        xg = const.tile([P, 4 * IN], BF16, align_bytes=64)
-        xq = const.tile([P, IN], U32, align_bytes=64)
-        xs = const.tile([P, IN], U8, align_bytes=64)
-        x32 = x_sb[:].bitcast(F32)
-        xg32 = xg[:].bitcast(F32).rearrange("p (g b c u) -> p g b c u", g=2, b=4, u=2)
-        out_rows = out.rearrange("(c t) o -> c t o", t=4)
+        bb_all = const.tile([P, HID], BF16)
 
-        banks = {}
-        w1g = {}
-        wbg = {}
-        w1q = {}
-        w1s = {}
-        wbq = {}
-        wbs = {}
-        hpl = {}
-        hg = {}
-        hq = {}
-        hs = {}
-        ot = {}
+        def spread_bb(n0, on_vector):
+            wide = psum.tile([P, 2 * CHUNK], BF16, tag="bank")
+            for s in range(2):
+                nc.tensor.matmul(out=wide[:, s * CHUNK:(s + 1) * CHUNK],
+                                 lhsT=ident_bf[:, n0 + s:n0 + s + 1].to_broadcast([P, P]),
+                                 rhs=bb_rows[:], start=True, stop=True)
+            copy_out(on_vector, bb_all[:, n0 * CHUNK:(n0 + 2) * CHUNK], wide[:])
 
-        def quarters(q):
-            if q == "all":
-                return 0, 4
-            if isinstance(q, str):
-                return int(q[0]), int(q[-1]) + 1
-            return q, q + 1
+        spread_bb(0, True)
+        spread_bb(2, False)
 
-        for op in ORDER:
-            f = op[0]
-            a = op[1]
-            if f == "BM":
-                wide = ring_v.tile([P, 2 * BLK], BF16, tag="bank")
-                banks[("bb", a)] = wide
-                for s in range(2):
-                    n = 2 * a + s
-                    nc.tensor.matmul(out=wide[:, s * BLK:(s + 1) * BLK], lhsT=identb[:, n:n + 1].to_broadcast([P, P]),
-                                     rhs=bbz[:], start=True, stop=True)
-            elif f == "BE":
-                copy_out(op[2], bbb[:, 2 * a * BLK:2 * (a + 1) * BLK], banks[("bb", a)][:])
-            elif f == "Tx":
-                banks[("x", a)] = transposes(x32, 512 * a)
-            elif f == "Ex":
-                copy_out(op[2], xg32[:, :, a, :, :], banks[("x", a)][:].rearrange("p (g u c) -> p g c u", g=2, u=2))
-            elif f == "Qx":
-                nc.vector.quantize_mx(out=xq[:, a * B:(a + 1) * B].bitcast(FP8X4), scales=xs[:, a * B:(a + 1) * B],
-                                      in_=xg[:, a * 4 * B:(a + 1) * 4 * B])
-            elif f == "T1":
-                banks[("w", a, op[2])] = transposes(w1_sbs[a][:].bitcast(F32), 512 * op[2])
-            elif f == "E1":
-                j = op[2]
-                if a not in w1g:
-                    w1g_t = work.tile([P, 4 * IN], BF16, align_bytes=64, bufs=2)
-                    w1g[a] = w1g_t
-                copy_out(op[3], w1g[a][:].bitcast(F32)[:, 512 * j:512 * (j + 1)].rearrange("p (g c u) -> p g c u", g=2, u=2),
-                         banks[("w", a, j)][:].rearrange("p (g u c) -> p g c u", g=2, u=2))
-            elif f == "QW":
-                w1q_t = work.tile([P, IN], U32, align_bytes=64, bufs=2)
-                w1s_t = work.tile([P, IN], U8, align_bytes=64, bufs=2)
-                w1q[a] = w1q_t
-                w1s[a] = w1s_t
-                nc.vector.quantize_mx(out=w1q_t[:].bitcast(FP8X4), scales=w1s_t[:], in_=w1g[a][:])
-            elif f == "TB":
-                banks[("b", a, op[2])] = transposes(wb_sbs[a][:].bitcast(F32), 512 * op[2])
-            elif f == "EB":
-                if a not in wbg:
-                    wbg_t = work.tile([P, 4 * BLK], BF16, align_bytes=64, bufs=2)
-                    wbg[a] = wbg_t
-                copy_out(op[3], wbg[a][:].bitcast(F32).rearrange("p (c h q) -> p c h q", h=2, q=4)[:, :, op[2], :],
-                         banks[("b", a, op[2])][:].rearrange("p (q c) -> p c q", q=4))
-            elif f == "QB":
-                wbq_t = work.tile([P, BLK], U32, align_bytes=64, bufs=3)
-                wbs_t = work.tile([P, BLK], U8, align_bytes=64, bufs=3)
-                wbq[a] = wbq_t
-                wbs[a] = wbs_t
-                nc.vector.quantize_mx(out=wbq_t[:].bitcast(FP8X4), scales=wbs_t[:], in_=wbg[a][:])
-            elif f == "M1":
-                j = op[2]
-                hp = ring_s.tile([P, B], F32, tag="bank")
-                banks[("h", a, j)] = hp
+        x_grouped = const.tile([P, TILES * K1], BF16, align_bytes=64)
+        x_codes = const.tile([P, K1], U32, align_bytes=64)
+        x_scales = const.tile([P, K1], U8, align_bytes=64)
+        x_words = x_sb[:].bitcast(F32)
+        x_pairs = x_grouped[:].bitcast(F32).rearrange("p (g b c u) -> p g b c u", g=2, b=TILES, u=2)
+        for b in range(TILES):
+            bank = transpose_words(x_words, BANK * b)
+            copy_out(b % 2 == 1, x_pairs[:, :, b, :, :], bank[:].rearrange("p (g u c) -> p g c u", g=2, u=2))
+        for g in range(2):
+            nc.vector.quantize_mx(out=x_codes[:, g * BATCH:(g + 1) * BATCH].bitcast(FP8X4),
+                                  scales=x_scales[:, g * BATCH:(g + 1) * BATCH],
+                                  in_=x_grouped[:, g * TILES * BATCH:(g + 1) * TILES * BATCH])
+
+        w1_grouped = {}
+        w1_codes = {}
+        w1_scales = {}
+        wb_grouped = {}
+        wb_codes = {}
+        wb_scales = {}
+        h_planes = {}
+        h_grouped = {}
+        h_codes = {}
+        h_scales = {}
+        products = {}
+        out_sb = {}
+        out_rows = out.rearrange("(c b) o -> c b o", b=TILES)
+
+        def transpose_w1(n):
+            grouped = work.tile([P, TILES * K1], BF16, align_bytes=64, tag="w1_grouped")
+            w1_grouped[n] = grouped
+            words = w1_sb[n][:].bitcast(F32)
+            pairs = grouped[:].bitcast(F32)
+            for t in range(TILES):
+                bank = transpose_words(words, BANK * t)
+                copy_out(n < HELPED and t % 2 == 1,
+                         pairs[:, BANK * t:BANK * (t + 1)].rearrange("p (g c u) -> p g c u", g=2, u=2),
+                         bank[:].rearrange("p (g u c) -> p g c u", g=2, u=2))
+
+        def quantise_w1(n):
+            codes = work.tile([P, K1], U32, align_bytes=64, tag="w1_codes")
+            scales = work.tile([P, K1], U8, align_bytes=64, tag="w1_scales")
+            w1_codes[n] = codes
+            w1_scales[n] = scales
+            nc.vector.quantize_mx(out=codes[:].bitcast(FP8X4), scales=scales[:], in_=w1_grouped[n][:])
+
+        def transpose_wb(n):
+            grouped = work.tile([P, TILES * CHUNK], BF16, align_bytes=64, tag="wb_grouped")
+            wb_grouped[n] = grouped
+            words = wb_sb[n][:].bitcast(F32)
+            pairs = grouped[:].bitcast(F32).rearrange("p (c hi lu) -> p c hi lu", hi=2, lu=4)
+            for hi in range(2):
+                bank = transpose_words(words, BANK * hi)
+                copy_out(n < HELPED, pairs[:, :, hi, :], bank[:].rearrange("p (lu c) -> p c lu", lu=4))
+
+        def quantise_wb(n):
+            codes = slow.tile([P, CHUNK], U32, align_bytes=64, tag="wb_codes")
+            scales = slow.tile([P, CHUNK], U8, align_bytes=64, tag="wb_scales")
+            wb_codes[n] = codes
+            wb_scales[n] = scales
+            nc.vector.quantize_mx(out=codes[:].bitcast(FP8X4), scales=scales[:], in_=wb_grouped[n][:])
+
+        def stage1(n):
+            planes = work.tile([P, TILES * BATCH], BF16, tag="h_planes")
+            h_planes[n] = planes
+            for t in range(TILES):
+                acc = psum.tile([P, BATCH], F32, tag="bank")
                 for g in range(2):
-                    lo = (2 * j + g) * P
-                    nc.tensor.matmul_mx(out=hp[:], lhsT=w1q[a][:, lo:lo + P].bitcast(FP8X4), lhsT_scale=w1s[a][:, lo:lo + P],
-                                        rhs=xq[:, g * B:(g + 1) * B].bitcast(FP8X4), rhs_scale=xs[:, g * B:(g + 1) * B],
+                    lo = (2 * t + g) * P
+                    nc.tensor.matmul_mx(out=acc[:], lhsT=w1_codes[n][:, lo:lo + P].bitcast(FP8X4),
+                                        lhsT_scale=w1_scales[n][:, lo:lo + P],
+                                        rhs=x_codes[:, g * BATCH:(g + 1) * BATCH].bitcast(FP8X4),
+                                        rhs_scale=x_scales[:, g * BATCH:(g + 1) * BATCH],
                                         start=(g == 0), stop=(g == 1))
-            elif f == "H":
-                j = op[2]
-                if a not in hpl:
-                    hpl_t = work.tile([P, 4 * B], BF16, bufs=2)
-                    hpl[a] = hpl_t
-                if op[3] == "v":
-                    nc.vector.tensor_scalar(out=hpl[a][:, j * B:(j + 1) * B], in0=banks[("h", a, j)][:],
-                                            scalar1=b1f[:, 4 * a + j:4 * a + j + 1], scalar2=0.0, op0=ALU.add, op1=ALU.max)
-                else:
-                    nc.scalar.activation(out=hpl[a][:, j * B:(j + 1) * B], in_=banks[("h", a, j)][:], func=RELU,
-                                         bias=b1f[:, 4 * a + j:4 * a + j + 1], scale=1.0)
-            elif f == "RG":
-                hg_t = work.tile([P, 4 * B], BF16, align_bytes=64, bufs=2)
-                hg[a] = hg_t
-                nc.vector.tensor_copy(out=hg_t[:].rearrange("p (c i t) -> p c t i", i=4, t=4),
-                                      in_=hpl[a][:].rearrange("p (t c i) -> p c t i", t=4, i=4))
-            elif f == "QH":
-                hq_t = work.tile([P, B], U32, align_bytes=64, bufs=2)
-                hs_t = work.tile([P, B], U8, align_bytes=64, bufs=2)
-                hq[a] = hq_t
-                hs[a] = hs_t
-                nc.vector.quantize_mx(out=hq_t[:].bitcast(FP8X4), scales=hs_t[:], in_=hg[a][:])
-            elif f == "M2":
-                bt = op[2]
-                acc = ring_v.tile([P, BLK], F32, tag="bank")
-                banks[("o", a, bt)] = acc
-                nc.tensor.matmul_mx(out=acc[:], lhsT=hq[a][:, bt * P:(bt + 1) * P].bitcast(FP8X4),
-                                    lhsT_scale=hs[a][:, bt * P:(bt + 1) * P],
-                                    rhs=wbq[a][:].bitcast(FP8X4), rhs_scale=wbs[a][:], start=True, stop=True)
-            elif f == "A":
-                bt = op[2]
-                if a not in ot:
-                    ot_t = work.tile([P, 4 * BLK], F32, bufs=3)
-                    ot[a] = ot_t
-                nc.vector.tensor_tensor(out=ot[a][:, bt * BLK:(bt + 1) * BLK], in0=banks[("o", a, bt)][:],
-                                        in1=bbb[:, a * BLK:(a + 1) * BLK], op=ALU.add)
-            elif f == "RL":
-                lo, hi = quarters(op[2])
-                part = ot[a][:, lo * BLK:hi * BLK]
-                if op[3] == "v":
-                    nc.vector.tensor_scalar_max(out=part, in0=part, scalar1=0.0)
-                elif op[3] == "s":
-                    nc.scalar.activation(out=part, in_=part, func=RELU)
-                else:
-                    nc.gpsimd.tensor_scalar(out=part, in0=part, scalar1=FLT_MAX, scalar2=0.0, op0=ALU.min, op1=ALU.max)
-            elif f == "ST":
-                lo, hi = quarters(op[2])
-                nc.sync.dma_start(out=out_rows[:, lo:hi, a * BLK:(a + 1) * BLK],
-                                  in_=ot[a][:].rearrange("p (t o) -> p t o", t=4)[:, lo:hi, :])
+                nc.scalar.activation(out=planes[:, t * BATCH:(t + 1) * BATCH], in_=acc[:], func=RELU,
+                                     bias=b1_col[:, TILES * n + t:TILES * n + t + 1], scale=1.0)
+
+        def regroup_h(n):
+            grouped = work.tile([P, TILES * BATCH], BF16, align_bytes=64, tag="h_grouped")
+            h_grouped[n] = grouped
+            nc.vector.tensor_copy(out=grouped[:].rearrange("p (run i t) -> p run t i", i=4, t=TILES),
+                                  in_=h_planes[n][:].rearrange("p (t run i) -> p run t i", t=TILES, i=4))
+
+        def quantise_h(n):
+            codes = work.tile([P, BATCH], U32, align_bytes=64, tag="h_codes")
+            scales = work.tile([P, BATCH], U8, align_bytes=64, tag="h_scales")
+            h_codes[n] = codes
+            h_scales[n] = scales
+            nc.vector.quantize_mx(out=codes[:].bitcast(FP8X4), scales=scales[:], in_=h_grouped[n][:])
+
+        def stage2(n):
+            for b in range(TILES):
+                acc = psum.tile([P, CHUNK], F32, tag="bank")
+                products[(n, b)] = acc
+                nc.tensor.matmul_mx(out=acc[:], lhsT=h_codes[n][:, b * P:(b + 1) * P].bitcast(FP8X4),
+                                    lhsT_scale=h_scales[n][:, b * P:(b + 1) * P],
+                                    rhs=wb_codes[n][:].bitcast(FP8X4), rhs_scale=wb_scales[n][:], start=True, stop=True)
+
+        def relu_and_store(n, first, last, on_vector):
+            part = out_sb[n][:, first * CHUNK:last * CHUNK]
+            if on_vector:
+                nc.vector.tensor_scalar_max(out=part, in0=part, scalar1=0.0)
+            else:
+                nc.scalar.activation(out=part, in_=part, func=RELU)
+            nc.sync.dma_start(out=out_rows[:, first:last, n * CHUNK:(n + 1) * CHUNK],
+                              in_=out_sb[n][:].rearrange("c (b o) -> c b o", b=TILES)[:, first:last, :])
+
+        def finish(n):
+            result = slow.tile([P, TILES * CHUNK], F32, tag="out_sb")
+            out_sb[n] = result
+            by_quarters = n in SCALAR_RELU or n == N_CHUNKS - 1
+            for b in range(TILES):
+                nc.vector.tensor_tensor(out=result[:, b * CHUNK:(b + 1) * CHUNK], in0=products[(n, b)][:],
+                                        in1=bb_all[:, n * CHUNK:(n + 1) * CHUNK], op=ADD)
+                if b == 1 and n + 1 < N_CHUNKS:
+                    quantise_h(n + 1)
+                if b == 0 or by_quarters:
+                    relu_and_store(n, b, b + 1, b > 0 and n not in SCALAR_RELU)
+            if not by_quarters:
+                relu_and_store(n, 1, TILES, True)
+
+        def exists(n):
+            return 0 <= n < N_CHUNKS
+
+        for p in range(-W1_AHEAD, N_CHUNKS):
+            if exists(p + W1_AHEAD):
+                transpose_w1(p + W1_AHEAD)
+            if exists(p + WB_AHEAD):
+                transpose_wb(p + WB_AHEAD)
+            if exists(p):
+                stage2(p)
+            if exists(p + STAGE1_AHEAD):
+                stage1(p + STAGE1_AHEAD)
+            if exists(p + 1):
+                regroup_h(p + 1)
+            if exists(p):
+                finish(p)
+            elif exists(p + 1):
+                quantise_h(p + 1)
+            if p in (1, 2):
+                spread_bb(2 * p + 2, False)
+            if exists(p + W1_AHEAD):
+                quantise_w1(p + W1_AHEAD)
+            if exists(p + WB_AHEAD):
+                quantise_wb(p + WB_AHEAD)

from contextlib import ExitStack

import concourse.mybir as mybir
from concourse.masks import make_identity

F32 = mybir.dt.float32
BF16 = mybir.dt.bfloat16
U32 = mybir.dt.uint32
U8 = mybir.dt.uint8
FP8X4 = mybir.dt.float8_e4m3fn_x4
RELU = mybir.ActivationFunctionType.Relu
ADD = mybir.AluOpType.add

P = 128
BATCH = 512
K1 = 1024
HID = 4096
CHUNK = 512
N_CHUNKS = HID // CHUNK
TILES = 4
BANK = 512
PSUM_BANKS = 8
W1_AHEAD = 3
WB_AHEAD = 2
STAGE1_AHEAD = 2
HELPED = 2
SCALAR_RELU = (5, 6)

FLOPS = 2 * BATCH * K1 * HID + 2 * BATCH * CHUNK * HID


def tile_blockdiagmnistconvertible_pa_kernel(tc, x, W1, b1, Wb, bb, out):
    nc = tc.nc
    with ExitStack() as ctx:
        const = ctx.enter_context(tc.tile_pool(name="const", bufs=1))
        w1_pool = ctx.enter_context(tc.tile_pool(name="w1_pool", bufs=N_CHUNKS))
        wb_pool = ctx.enter_context(tc.tile_pool(name="wb_pool", bufs=N_CHUNKS))
        work = ctx.enter_context(tc.tile_pool(name="work", bufs=2))
        slow = ctx.enter_context(tc.tile_pool(name="slow", bufs=3))
        psum = ctx.enter_context(tc.psum_pool(name="psum", bufs=PSUM_BANKS))
        ctx.enter_context(tc.manual_schedule())

        ident = const.tile([P, P], F32)
        make_identity(nc, ident[:])
        b1_rows = const.tile([P, 2 * P], BF16)
        nc.vector.memset(b1_rows[:], 0.0)
        bb_rows = const.tile([P, CHUNK], BF16)
        nc.vector.memset(bb_rows[:], 0.0)
        nc.sync.dma_start(out=b1_rows[0:2 * N_CHUNKS, :], in_=b1.rearrange("(r w) -> r w", w=2 * P))
        nc.sync.dma_start(out=bb_rows[0:N_CHUNKS, :], in_=bb.rearrange("(n o) -> n o", o=CHUNK))

        x_sb = const.tile([P, TILES * K1], BF16)
        x_src = x.rearrange("(c b) k -> c b k", b=TILES)
        x_dst = x_sb[:].rearrange("c (b k) -> c b k", b=TILES)
        for half in range(2):
            nc.sync.dma_start(out=x_dst[:, 2 * half:2 * half + 2, :], in_=x_src[:, 2 * half:2 * half + 2, :])

        w1_sb = {}
        wb_sb = {}

        def load_w1(n):
            w1_tile = w1_pool.tile([P, TILES * K1], BF16)
            w1_sb[n] = w1_tile
            src = W1[n * CHUNK:(n + 1) * CHUNK, :].rearrange("(u p e) k -> p u e k", u=2, p=P, e=2)
            dst = w1_tile[:].rearrange("p (u e k) -> p u e k", u=2, e=2)
            if n == 0:
                for u in range(2):
                    nc.sync.dma_start(out=dst[:, u, :, :], in_=src[:, u, :, :])
            else:
                nc.sync.dma_start(out=dst, in_=src)

        def load_wb(n):
            wb_tile = wb_pool.tile([P, TILES * CHUNK], BF16)
            wb_sb[n] = wb_tile
            nc.sync.dma_start(out=wb_tile[:].rearrange("c (j k) -> c j k", j=TILES),
                              in_=Wb[n].rearrange("(c j) k -> c j k", j=TILES))

        load_w1(0)
        for n in range(1, N_CHUNKS):
            load_w1(n)
            load_wb(n - 1)
        load_wb(N_CHUNKS - 1)

        ident_bf = const.tile([P, P], BF16)
        nc.vector.tensor_copy(out=ident_bf[:], in_=ident[:])

        def copy_out(on_vector, dst, src):
            if on_vector:
                nc.vector.tensor_copy(out=dst, in_=src)
            else:
                nc.scalar.copy(out=dst, in_=src)

        def transpose_words(words, first):
            bank = psum.tile([P, BANK], F32, tag="bank")
            for i in range(4):
                lo = first + P * i
                nc.tensor.transpose(out=bank[:, P * i:P * (i + 1)], in_=words[:, lo:lo + P], identity=ident[:])
            return bank

        b1_bank = psum.tile([P, BANK], F32, tag="bank")
        nc.tensor.transpose(out=b1_bank[:, 0:P], in_=b1_rows[:].bitcast(F32), identity=ident[:])
        b1_words = const.tile([P, 2 * N_CHUNKS], F32)
        nc.vector.tensor_copy(out=b1_words[:], in_=b1_bank[:, 0:2 * N_CHUNKS])
        b1_col = const.tile([P, TILES * N_CHUNKS], F32)
        nc.vector.tensor_copy(out=b1_col[:], in_=b1_words[:].bitcast(BF16))

        bb_all = const.tile([P, HID], BF16)

        def spread_bb(n0, on_vector):
            wide = psum.tile([P, 2 * CHUNK], BF16, tag="bank")
            for s in range(2):
                nc.tensor.matmul(out=wide[:, s * CHUNK:(s + 1) * CHUNK],
                                 lhsT=ident_bf[:, n0 + s:n0 + s + 1].to_broadcast([P, P]),
                                 rhs=bb_rows[:], start=True, stop=True)
            copy_out(on_vector, bb_all[:, n0 * CHUNK:(n0 + 2) * CHUNK], wide[:])

        spread_bb(0, True)
        spread_bb(2, False)

        x_grouped = const.tile([P, TILES * K1], BF16, align_bytes=64)
        x_codes = const.tile([P, K1], U32, align_bytes=64)
        x_scales = const.tile([P, K1], U8, align_bytes=64)
        x_words = x_sb[:].bitcast(F32)
        x_pairs = x_grouped[:].bitcast(F32).rearrange("p (g b c u) -> p g b c u", g=2, b=TILES, u=2)
        for b in range(TILES):
            bank = transpose_words(x_words, BANK * b)
            copy_out(b % 2 == 1, x_pairs[:, :, b, :, :], bank[:].rearrange("p (g u c) -> p g c u", g=2, u=2))
        for g in range(2):
            nc.vector.quantize_mx(out=x_codes[:, g * BATCH:(g + 1) * BATCH].bitcast(FP8X4),
                                  scales=x_scales[:, g * BATCH:(g + 1) * BATCH],
                                  in_=x_grouped[:, g * TILES * BATCH:(g + 1) * TILES * BATCH])

        w1_grouped = {}
        w1_codes = {}
        w1_scales = {}
        wb_grouped = {}
        wb_codes = {}
        wb_scales = {}
        h_planes = {}
        h_grouped = {}
        h_codes = {}
        h_scales = {}
        products = {}
        out_sb = {}
        out_rows = out.rearrange("(c b) o -> c b o", b=TILES)

        def transpose_w1(n):
            grouped = work.tile([P, TILES * K1], BF16, align_bytes=64, tag="w1_grouped")
            w1_grouped[n] = grouped
            words = w1_sb[n][:].bitcast(F32)
            pairs = grouped[:].bitcast(F32)
            for t in range(TILES):
                bank = transpose_words(words, BANK * t)
                copy_out(n < HELPED and t % 2 == 1,
                         pairs[:, BANK * t:BANK * (t + 1)].rearrange("p (g c u) -> p g c u", g=2, u=2),
                         bank[:].rearrange("p (g u c) -> p g c u", g=2, u=2))

        def quantise_w1(n):
            codes = work.tile([P, K1], U32, align_bytes=64, tag="w1_codes")
            scales = work.tile([P, K1], U8, align_bytes=64, tag="w1_scales")
            w1_codes[n] = codes
            w1_scales[n] = scales
            nc.vector.quantize_mx(out=codes[:].bitcast(FP8X4), scales=scales[:], in_=w1_grouped[n][:])

        def transpose_wb(n):
            grouped = work.tile([P, TILES * CHUNK], BF16, align_bytes=64, tag="wb_grouped")
            wb_grouped[n] = grouped
            words = wb_sb[n][:].bitcast(F32)
            pairs = grouped[:].bitcast(F32).rearrange("p (c hi lu) -> p c hi lu", hi=2, lu=4)
            for hi in range(2):
                bank = transpose_words(words, BANK * hi)
                copy_out(n < HELPED, pairs[:, :, hi, :], bank[:].rearrange("p (lu c) -> p c lu", lu=4))

        def quantise_wb(n):
            codes = slow.tile([P, CHUNK], U32, align_bytes=64, tag="wb_codes")
            scales = slow.tile([P, CHUNK], U8, align_bytes=64, tag="wb_scales")
            wb_codes[n] = codes
            wb_scales[n] = scales
            nc.vector.quantize_mx(out=codes[:].bitcast(FP8X4), scales=scales[:], in_=wb_grouped[n][:])

        def stage1(n):
            planes = work.tile([P, TILES * BATCH], BF16, tag="h_planes")
            h_planes[n] = planes
            for t in range(TILES):
                acc = psum.tile([P, BATCH], F32, tag="bank")
                for g in range(2):
                    lo = (2 * t + g) * P
                    nc.tensor.matmul_mx(out=acc[:], lhsT=w1_codes[n][:, lo:lo + P].bitcast(FP8X4),
                                        lhsT_scale=w1_scales[n][:, lo:lo + P],
                                        rhs=x_codes[:, g * BATCH:(g + 1) * BATCH].bitcast(FP8X4),
                                        rhs_scale=x_scales[:, g * BATCH:(g + 1) * BATCH],
                                        start=(g == 0), stop=(g == 1))
                nc.scalar.activation(out=planes[:, t * BATCH:(t + 1) * BATCH], in_=acc[:], func=RELU,
                                     bias=b1_col[:, TILES * n + t:TILES * n + t + 1], scale=1.0)

        def regroup_h(n):
            grouped = work.tile([P, TILES * BATCH], BF16, align_bytes=64, tag="h_grouped")
            h_grouped[n] = grouped
            nc.vector.tensor_copy(out=grouped[:].rearrange("p (run i t) -> p run t i", i=4, t=TILES),
                                  in_=h_planes[n][:].rearrange("p (t run i) -> p run t i", t=TILES, i=4))

        def quantise_h(n):
            codes = work.tile([P, BATCH], U32, align_bytes=64, tag="h_codes")
            scales = work.tile([P, BATCH], U8, align_bytes=64, tag="h_scales")
            h_codes[n] = codes
            h_scales[n] = scales
            nc.vector.quantize_mx(out=codes[:].bitcast(FP8X4), scales=scales[:], in_=h_grouped[n][:])

        def stage2(n):
            for b in range(TILES):
                acc = psum.tile([P, CHUNK], F32, tag="bank")
                products[(n, b)] = acc
                nc.tensor.matmul_mx(out=acc[:], lhsT=h_codes[n][:, b * P:(b + 1) * P].bitcast(FP8X4),
                                    lhsT_scale=h_scales[n][:, b * P:(b + 1) * P],
                                    rhs=wb_codes[n][:].bitcast(FP8X4), rhs_scale=wb_scales[n][:], start=True, stop=True)

        def relu_and_store(n, first, last, on_vector):
            part = out_sb[n][:, first * CHUNK:last * CHUNK]
            if on_vector:
                nc.vector.tensor_scalar_max(out=part, in0=part, scalar1=0.0)
            else:
                nc.scalar.activation(out=part, in_=part, func=RELU)
            nc.sync.dma_start(out=out_rows[:, first:last, n * CHUNK:(n + 1) * CHUNK],
                              in_=out_sb[n][:].rearrange("c (b o) -> c b o", b=TILES)[:, first:last, :])

        def finish(n):
            result = slow.tile([P, TILES * CHUNK], F32, tag="out_sb")
            out_sb[n] = result
            by_quarters = n in SCALAR_RELU or n == N_CHUNKS - 1
            for b in range(TILES):
                nc.vector.tensor_tensor(out=result[:, b * CHUNK:(b + 1) * CHUNK], in0=products[(n, b)][:],
                                        in1=bb_all[:, n * CHUNK:(n + 1) * CHUNK], op=ADD)
                if b == 1 and n + 1 < N_CHUNKS:
                    quantise_h(n + 1)
                if b == 0 or by_quarters:
                    relu_and_store(n, b, b + 1, b > 0 and n not in SCALAR_RELU)
            if not by_quarters:
                relu_and_store(n, 1, TILES, True)

        def exists(n):
            return 0 <= n < N_CHUNKS

        for p in range(-W1_AHEAD, N_CHUNKS):
            if exists(p + W1_AHEAD):
                transpose_w1(p + W1_AHEAD)
            if exists(p + WB_AHEAD):
                transpose_wb(p + WB_AHEAD)
            if exists(p):
                stage2(p)
            if exists(p + STAGE1_AHEAD):
                stage1(p + STAGE1_AHEAD)
            if exists(p + 1):
                regroup_h(p + 1)
            if exists(p):
                finish(p)
            elif exists(p + 1):
                quantise_h(p + 1)
            if p in (1, 2):
                spread_bb(2 * p + 2, False)
            if exists(p + W1_AHEAD):
                quantise_w1(p + W1_AHEAD)
            if exists(p + WB_AHEAD):
                quantise_wb(p + WB_AHEAD)
